import numpy as np
import ml_dtypes


def mxq(x, axis, fmt="e4m3"):
    dtype, down = {"e4m3": (ml_dtypes.float8_e4m3fn, 7), "e5m2": (ml_dtypes.float8_e5m2, 14)}[fmt]
    v = np.moveaxis(np.asarray(x, np.float32).astype(ml_dtypes.bfloat16).astype(np.float64), axis, -1)
    blocks = v.reshape(v.shape[:-1] + (-1, 32))
    amax = np.abs(blocks).max(-1, keepdims=True)
    byte = np.maximum(np.where(amax > 0, np.frexp(amax)[1] - 1 + 127, 0) - down, 1)
    scale = np.exp2(byte - 127.0)
    codes = (blocks / scale).astype(np.float32).astype(dtype).astype(np.float64)
    return np.moveaxis((codes * scale).reshape(v.shape), -1, axis)


WIDE = False


def mx_kscale(k):
    if not WIDE:
        return np.ones(k)
    levels = np.array([10, -10, 5, -5, 0])
    if k % 512:
        return np.exp2(np.random.permutation(np.resize(levels, k // 32))).repeat(32)
    a = np.empty((k // 512, 16))
    for p in range(k // 512):
        a[p, :8] = np.random.permutation(np.resize(levels, 8))
        for g in range(8):
            far = levels[np.abs(levels - a[p, g]) >= 10]
            a[p, g + 8] = far[np.random.randint(len(far))]
    return np.exp2(a.ravel()).repeat(32)


BF16 = ml_dtypes.bfloat16


def bf(x):
    return np.asarray(x, np.float32).astype(BF16)


def f64(x):
    return np.asarray(x).astype(np.float64)


B, N, D, GROUP, E1, S1, E2, HID = 4, 32768, 512, 512, 8, 8, 2, 1024
G = N // GROUP
NS = S1 // E2
M = S1 // NS
P2 = E2 * M
R = B * G * M
EPS = 1e-6
LG = 2.0


def l2norm(t):
    return t / np.sqrt(np.sum(t * t, axis=-1, keepdims=True) + EPS)


def setup_inputs():
    s = mx_kscale(D)
    c = np.sqrt(np.mean(1.0 / s**2))
    y = LG / np.sqrt(D) * np.random.standard_normal((B, G, E1, S1, D)) * s * c
    return {"yn": bf(y),
            "means": bf(y.reshape(B, G, E1, M, NS, D).mean(axis=4)),
            "w_slot2": bf(np.random.standard_normal((E1, D, E2 * D)) / s[:, None] / np.tile(s, E2))}


def reference(yn, means, w_slot2):
    mk = f64(means).transpose(2, 0, 1, 3, 4).reshape(E1, R, D)
    se = mxq(mk, 2, "e4m3") @ mxq(f64(w_slot2), 1, "e4m3")
    se = se.reshape(E1, B, G, M, E2, D).transpose(1, 2, 0, 4, 3, 5)
    se2 = (l2norm(se) * np.sqrt(D)).reshape(B, G, E1, P2, D)
    logits = mxq(f64(yn), 4, "e4m3") @ mxq(se2, 4, "e4m3").swapaxes(3, 4)
    a = np.exp(logits - logits.max(axis=3, keepdims=True))
    disp2 = a / a.sum(axis=3, keepdims=True)
    c = np.exp(logits - logits.max(axis=4, keepdims=True))
    comb2 = c / c.sum(axis=4, keepdims=True)
    return disp2, comb2

@@ -1,0 +1,443 @@
+from contextlib import ExitStack
+
+import concourse.mybir as mybir
+from concourse.masks import make_identity
+
+F32 = mybir.dt.float32
+BF16 = mybir.dt.bfloat16
+U32 = mybir.dt.uint32
+U8 = mybir.dt.uint8
+FP8X4 = mybir.dt.float8_e4m3fn_x4
+ALU = mybir.AluOpType
+ACT = mybir.ActivationFunctionType
+AXIS = mybir.AxisListType
+
+P = 128
+PACK = 4
+EXPERTS = 8
+GROUPS = 256
+HALVES = GROUPS // P
+TOKENS = 8
+SEGMENTS = 2
+INNER = 2
+SLOTS = INNER * SEGMENTS
+D = 512
+WORDS = D // 2
+T = 16
+B = GROUPS // T
+LO = B // HALVES
+BANK = 512
+PAIRS = HALVES * SEGMENTS * INNER
+PER_BANK = BANK // P
+EPS = 1e-6
+
+FLOPS = 2 * EXPERTS * GROUPS * SEGMENTS * D * INNER * D + 2 * EXPERTS * GROUPS * TOKENS * SLOTS * D
+
+
+def tile_hierarchicalsoftmoe2dblock_pb_t_kernel(tc, yn, means, w_slot2, out_0, out_1):
+    nc = tc.nc
+    yn_rows = yn.rearrange("b g k s d -> k (b g) (s d)")
+    means_rows = means.rearrange("b g k m d -> k (b g) (m d)")
+
+    with ExitStack() as ctx:
+        consts = ctx.enter_context(tc.tile_pool(name="consts", bufs=1))
+        first_in = ctx.enter_context(tc.tile_pool(name="first_in", bufs=2))
+        token_in = ctx.enter_context(tc.tile_pool(name="token_in", bufs=2 * HALVES))
+        grouped = ctx.enter_context(tc.tile_pool(name="grouped", bufs=2))
+        packed_first = ctx.enter_context(tc.tile_pool(name="packed_first", bufs=3))
+        packed_second = ctx.enter_context(tc.tile_pool(name="packed_second", bufs=2))
+        norms = ctx.enter_context(tc.tile_pool(name="norms", bufs=2))
+        unread = ctx.enter_context(tc.tile_pool(name="unread", bufs=4))
+        picked = ctx.enter_context(tc.tile_pool(name="picked", bufs=2))
+        last = ctx.enter_context(tc.tile_pool(name="last", bufs=1))
+        turned_ps = ctx.enter_context(tc.psum_pool(name="turned_ps", bufs=2))
+        rows_ps = ctx.enter_context(tc.psum_pool(name="rows_ps", bufs=2))
+        cols_ps = ctx.enter_context(tc.psum_pool(name="cols_ps", bufs=2))
+        spread_ps = ctx.enter_context(tc.psum_pool(name="spread_ps", bufs=1))
+        logit_ps = ctx.enter_context(tc.psum_pool(name="logit_ps", bufs=1))
+        ctx.enter_context(tc.manual_schedule())
+
+        ident = consts.tile([P, P], F32)
+        make_identity(nc, ident[:])
+        by_t = consts.tile([P, P], F32)
+        nc.vector.tensor_copy(
+            out=by_t[:].rearrange("i (t lo) -> i t lo", t=T),
+            in_=ident[:].rearrange("i (lo t) -> i t lo", t=T),
+        )
+        own_group = consts.tile([P, B], F32)
+        nc.vector.tensor_reduce(
+            out=own_group[:], in_=ident[:].rearrange("q (s b) -> q b s", b=B), axis=AXIS.X, op=ALU.add
+        )
+        logits = consts.tile([P, SLOTS, T * EXPERTS], F32)
+
+        w_raw, m_raw, y_raw = {}, {}, {}
+        m_grouped, w_grouped, y_grouped, s_grouped = {}, {}, {}, {}
+        w_codes, w_scales, m_codes, m_scales = {}, {}, {}, {}
+        y_codes, y_scales, s_codes, s_scales = {}, {}, {}, {}
+        square_sums, link, inv_norm_all = {}, {}, {}
+
+        def exists(k):
+            return 0 <= k < EXPERTS
+
+        def load_first(k):
+            if not exists(k):
+                return
+            w_in = first_in.tile([P, PACK, INNER * D], BF16)
+            nc.sync.dma_start(out=w_in[:], in_=w_slot2[k].rearrange("(p j) c -> p j c", j=PACK))
+            m_in = first_in.tile([P, HALVES, SEGMENTS * D], BF16)
+            nc.sync.dma_start(out=m_in[:], in_=means_rows[k].rearrange("(h p) x -> p h x", p=P))
+            m_raw[k], w_raw[k] = m_in, w_in
+
+        def load_tokens(k):
+            if not exists(k):
+                return
+            y_raw[k] = []
+            for half in range(HALVES):
+                y_in = token_in.tile([P, TOKENS * D], BF16)
+                nc.sync.dma_start(out=y_in[:], in_=yn_rows[k, half * P : (half + 1) * P, :])
+                y_raw[k].append(y_in)
+
+        def copy_turned(filling, out, in_):
+            if filling:
+                nc.vector.tensor_copy(out=out, in_=in_)
+            else:
+                nc.scalar.copy(out=out, in_=in_)
+
+        def turn_means(k, half, filling):
+            if not exists(k):
+                return
+            if half == 0:
+                m_new = grouped.tile([P, HALVES * SEGMENTS * P * PACK], BF16, align_bytes=64, name="m_grouped")
+                m_grouped[k] = m_new
+            m_pairs = m_grouped[k][:].bitcast(F32).rearrange("p (g c u) -> p g c u", c=P, u=2)
+            m_words = m_raw[k][:].bitcast(F32)
+            turned = turned_ps.tile([P, SEGMENTS, 2, P], F32)
+            for m in range(SEGMENTS):
+                for u in range(2):
+                    every_second = slice(m * WORDS + u, (m + 1) * WORDS, 2)
+                    nc.tensor.transpose(turned[:, m, u, :], m_words[:, half, every_second], by_t[:])
+            copy_turned(
+                filling,
+                out=m_pairs[:, SEGMENTS * half : SEGMENTS * (half + 1), :, :],
+                in_=turned[:].rearrange("p m u c -> p m c u"),
+            )
+
+        def quantise_means(k):
+            if not exists(k):
+                return
+            codes = packed_first.tile([P, HALVES * SEGMENTS * P], U32, align_bytes=64, name="m_codes")
+            scales = packed_first.tile([P, HALVES * SEGMENTS * P], U8, align_bytes=64, name="m_scales")
+            nc.vector.quantize_mx(out=codes[:].bitcast(FP8X4), scales=scales[:], in_=m_grouped[k][:])
+            m_codes[k], m_scales[k] = codes, scales
+
+        def regroup_w(k, a):
+            if not exists(k):
+                return
+            if a == 0:
+                w_new = grouped.tile([P, INNER * D * PACK], BF16, align_bytes=64, name="w_grouped")
+                w_grouped[k] = w_new
+            dst = w_grouped[k][:].rearrange("p (a odd q j) -> p a q odd j", a=2 * INNER, odd=2, j=PACK)
+            src = w_raw[k][:].rearrange("p j (e q u odd) -> p e u q odd j", e=INNER, u=2, odd=2)
+            if a % 2 == 0:
+                nc.vector.tensor_copy(out=dst[:, a], in_=src[:, a // 2, a % 2])
+            else:
+                nc.scalar.copy(out=dst[:, a], in_=src[:, a // 2, a % 2])
+
+        def quantise_w(k, e):
+            if not exists(k):
+                return
+            if e == 0:
+                codes = packed_first.tile([P, INNER * D], U32, align_bytes=64, name="w_codes")
+                scales = packed_first.tile([P, INNER * D], U8, align_bytes=64, name="w_scales")
+                w_codes[k], w_scales[k] = codes, scales
+            nc.vector.quantize_mx(
+                out=w_codes[k][:, e * D : (e + 1) * D].bitcast(FP8X4),
+                scales=w_scales[k][:, e * D : (e + 1) * D],
+                in_=w_grouped[k][:, e * D * PACK : (e + 1) * D * PACK],
+            )
+
+        def turn_tokens(k, i, filling):
+            if not exists(k):
+                return
+            half, s0 = i // (TOKENS // 2), 2 * (i % (TOKENS // 2))
+            if i == 0:
+                y_new = grouped.tile([P, T * TOKENS * B * PACK], BF16, align_bytes=64, name="y_grouped")
+                y_grouped[k] = y_new
+            y_pairs = y_grouped[k][:].bitcast(F32).rearrange("p (t s b u) -> p s t b u", t=T, s=TOKENS, u=2)
+            y_words = y_raw[k][half][:].bitcast(F32)
+            turned = turned_ps.tile([P, 2, 2, P], F32)
+            for s in range(2):
+                for u in range(2):
+                    every_second = slice((s0 + s) * WORDS + u, (s0 + s + 1) * WORDS, 2)
+                    nc.tensor.transpose(turned[:, s, u, :], y_words[:, every_second], by_t[:])
+            copy_turned(
+                filling,
+                out=y_pairs[:, s0 : s0 + 2, :, LO * half : LO * (half + 1), :],
+                in_=turned[:].rearrange("p s u (t lo) -> p s t lo u", t=T),
+            )
+
+        def quantise_tokens(k, part):
+            if not exists(k):
+                return
+            if part == 0:
+                codes = packed_second.tile([P, T * P], U32, align_bytes=64, name="y_codes")
+                scales = packed_second.tile([P, T * P], U8, align_bytes=64, name="y_scales")
+                y_codes[k], y_scales[k] = codes, scales
+            width = T * P // 2
+            nc.vector.quantize_mx(
+                out=y_codes[k][:, part * width : (part + 1) * width].bitcast(FP8X4),
+                scales=y_scales[k][:, part * width : (part + 1) * width],
+                in_=y_grouped[k][:, part * width * PACK : (part + 1) * width * PACK],
+            )
+
+        def sum_squares(k, i):
+            if not exists(k):
+                return
+            e, g = i // PER_BANK, i % PER_BANK
+            if i == 0:
+                sums = norms.tile([P, PAIRS], F32)
+                square_sums[k] = sums
+            se_rows = rows_ps.tile([P, D], F32)
+            nc.tensor.matmul_mx(
+                out=se_rows[:],
+                lhsT=m_codes[k][:, g * P : (g + 1) * P].bitcast(FP8X4),
+                lhsT_scale=m_scales[k][:, g * P : (g + 1) * P],
+                rhs=w_codes[k][:, e * D : (e + 1) * D].bitcast(FP8X4),
+                rhs_scale=w_scales[k][:, e * D : (e + 1) * D],
+                start=True,
+                stop=True,
+            )
+            squares = unread.tile([P, D], BF16)
+            nc.scalar.activation(
+                out=squares[:], in_=se_rows[:], func=ACT.Square, accum_out=square_sums[k][:, i : i + 1]
+            )
+
+        def mean_squares(k, part):
+            if not exists(k):
+                return
+            mean_sq = norms.tile([P, PER_BANK], F32)
+            nc.vector.tensor_scalar(
+                out=mean_sq[:],
+                in0=square_sums[k][:, part * PER_BANK : (part + 1) * PER_BANK],
+                scalar1=EPS,
+                scalar2=1.0 / D,
+                op0=ALU.add,
+                op1=ALU.mult,
+            )
+            link[k, part] = mean_sq
+
+        def roots(k, part):
+            if not exists(k):
+                return
+            rms = norms.tile([P, PER_BANK], F32)
+            nc.scalar.sqrt(out=rms[:], in_=link[k, part][:])
+            link[k, part] = rms
+
+        def inverses(k, part):
+            if not exists(k):
+                return
+            inv_norm = norms.tile([P, PER_BANK], F32)
+            nc.vector.reciprocal(out=inv_norm[:], in_=link[k, part][:])
+            link[k, part] = inv_norm
+
+        def spread_norms(k, part):
+            if not exists(k):
+                return
+            if part == 0:
+                everywhere = norms.tile([P, PAIRS, P], F32)
+                inv_norm_all[k] = everywhere
+            spread = spread_ps.tile([P, PER_BANK, P], F32)
+            for i in range(PER_BANK):
+                nc.tensor.transpose(spread[:, i, :], link[k, part][:, i : i + 1].to_broadcast([P, P]), ident[:])
+            nc.scalar.copy(out=inv_norm_all[k][:, part * PER_BANK : (part + 1) * PER_BANK, :], in_=spread[:])
+
+        def make_slots(k, i):
+            if not exists(k):
+                return
+            e, g = i // PER_BANK, i % PER_BANK
+            half, m = g // SEGMENTS, g % SEGMENTS
+            if i == 0:
+                s_new = grouped.tile([P, T * SLOTS * B * PACK], BF16, align_bytes=64, name="s_grouped")
+                s_grouped[k] = s_new
+            se_cols = cols_ps.tile([P, PACK, P], F32)
+            for j in range(PACK):
+                chunk = slice((PACK * e + j) * P, (PACK * e + j + 1) * P)
+                nc.tensor.matmul_mx(
+                    out=se_cols[:, j, :],
+                    lhsT=w_codes[k][:, chunk].bitcast(FP8X4),
+                    lhsT_scale=w_scales[k][:, chunk],
+                    rhs=m_codes[k][:, g * P : (g + 1) * P].bitcast(FP8X4),
+                    rhs_scale=m_scales[k][:, g * P : (g + 1) * P],
+                    start=True,
+                    stop=True,
+                )
+            by_column = s_grouped[k][:].rearrange("p (t slot b j) -> p slot t b j", t=T, slot=SLOTS, j=PACK)
+            scale = inv_norm_all[k][:, i, :].rearrange("p (t lo) -> p t lo", t=T)
+            nc.vector.tensor_tensor(
+                out=by_column[:, SEGMENTS * e + m, :, LO * half : LO * (half + 1), :],
+                in0=se_cols[:].rearrange("p j (t lo) -> p t lo j", t=T),
+                in1=scale.unsqueeze(3).to_broadcast([P, T, LO, PACK]),
+                op=ALU.mult,
+            )
+
+        def quantise_slots(k, part):
+            if not exists(k):
+                return
+            if part == 0:
+                codes = packed_second.tile([P, T * SLOTS * B], U32, align_bytes=64, name="s_codes")
+                scales = packed_second.tile([P, T * SLOTS * B], U8, align_bytes=64, name="s_scales")
+                s_codes[k], s_scales[k] = codes, scales
+            width = T * SLOTS * B // 2
+            nc.vector.quantize_mx(
+                out=s_codes[k][:, part * width : (part + 1) * width].bitcast(FP8X4),
+                scales=s_scales[k][:, part * width : (part + 1) * width],
+                in_=s_grouped[k][:, part * width * PACK : (part + 1) * width * PACK],
+            )
+
+        def cross(k, part):
+            if not exists(k):
+                return
+            t0 = part * T // 2
+            crossed = logit_ps.tile([P, T // 2, SLOTS * B], F32)
+            for i in range(T // 2):
+                t = t0 + i
+                nc.tensor.matmul_mx(
+                    out=crossed[:, i, :],
+                    lhsT=y_codes[k][:, t * P : (t + 1) * P].bitcast(FP8X4),
+                    lhsT_scale=y_scales[k][:, t * P : (t + 1) * P],
+                    rhs=s_codes[k][:, t * SLOTS * B : (t + 1) * SLOTS * B].bitcast(FP8X4),
+                    rhs_scale=s_scales[k][:, t * SLOTS * B : (t + 1) * SLOTS * B],
+                    start=True,
+                    stop=True,
+                )
+            return crossed
+
+        def pick(k, part, crossed):
+            if not exists(k):
+                return
+            t0 = part * T // 2
+            own = picked.tile([P, T // 2 * SLOTS, B], F32)
+            nc.vector.tensor_tensor(
+                out=own[:],
+                in0=crossed[:].rearrange("q t (slot b) -> q (t slot) b", b=B),
+                in1=own_group[:].unsqueeze(1).to_broadcast([P, T // 2 * SLOTS, B]),
+                op=ALU.mult,
+            )
+            nc.vector.tensor_reduce(
+                out=logits[:].rearrange("q slot (t k) -> q slot t k", k=EXPERTS)[:, :, t0 : t0 + T // 2, k],
+                in_=own[:].rearrange("q (t slot) b -> q slot t b", slot=SLOTS),
+                axis=AXIS.X,
+                op=ALU.add,
+            )
+
+        load_first(0)
+        load_tokens(0)
+        load_first(1)
+        for k in range(-2, EXPERTS + 1):
+            filling = k < 0
+
+            make_slots(k, 0)
+            sum_squares(k + 1, 0)
+            turn_tokens(k + 1, 0, filling)
+            mean_squares(k, 1)
+            quantise_slots(k - 1, 0)
+            regroup_w(k + 2, 0)
+
+            make_slots(k, 1)
+            sum_squares(k + 1, 1)
+            crossed = cross(k - 1, 0)
+            turn_tokens(k + 1, 1, filling)
+            roots(k, 1)
+            quantise_slots(k - 1, 1)
+            regroup_w(k + 2, 1)
+
+            make_slots(k, 2)
+            sum_squares(k + 1, 2)
+            turn_tokens(k + 1, 2, filling)
+            inverses(k, 1)
+            quantise_tokens(k, 0)
+            regroup_w(k + 2, 2)
+
+            make_slots(k, 3)
+            sum_squares(k + 1, 3)
+            turn_tokens(k + 1, 3, filling)
+            spread_norms(k, 1)
+            pick(k - 1, 0, crossed)
+            regroup_w(k + 2, 3)
+
+            make_slots(k, 4)
+            sum_squares(k + 1, 4)
+            crossed = cross(k - 1, 1)
+            turn_tokens(k + 1, 4, filling)
+            turn_means(k + 2, 0, filling)
+            mean_squares(k + 1, 0)
+            quantise_tokens(k, 1)
+
+            make_slots(k, 5)
+            sum_squares(k + 1, 5)
+            turn_tokens(k + 1, 5, filling)
+            turn_means(k + 2, 1, filling)
+            roots(k + 1, 0)
+            quantise_w(k + 2, 0)
+
+            make_slots(k, 6)
+            sum_squares(k + 1, 6)
+            turn_tokens(k + 1, 6, filling)
+            inverses(k + 1, 0)
+            pick(k - 1, 1, crossed)
+
+            make_slots(k, 7)
+            sum_squares(k + 1, 7)
+            turn_tokens(k + 1, 7, filling)
+            spread_norms(k + 1, 0)
+            quantise_means(k + 2)
+            quantise_w(k + 2, 1)
+
+            load_tokens(k + 3)
+            load_first(k + 4)
+
+        by_row_ps = logit_ps.tile([P, SLOTS, P], F32, tag="crossed")
+        for slot in range(SLOTS):
+            nc.tensor.transpose(by_row_ps[:, slot, :], logits[:, slot, :], ident[:])
+        by_row = by_row_ps[:].rearrange("r slot (s b) -> r slot s b", b=B)
+        full = [P, SLOTS, TOKENS, B]
+        over_tokens = (
+            out_0,
+            lambda x: x.rearrange("r slot s b -> r slot b s"),
+            [P, SLOTS, B],
+            lambda x: x.unsqueeze(2).to_broadcast(full),
+        )
+        over_slots = (
+            out_1,
+            lambda x: x.rearrange("r slot s b -> r s b slot"),
+            [P, TOKENS, B],
+            lambda x: x.unsqueeze(1).to_broadcast(full),
+        )
+        both = (over_tokens, over_slots)
+        tops, shifteds, totals = [], [], []
+        for out, index_last, reduced_shape, repeated in both:
+            top = last.tile(reduced_shape, F32, bufs=2)
+            nc.vector.tensor_reduce(out=top[:], in_=index_last(by_row), axis=AXIS.X, op=ALU.max)
+            tops.append(top)
+        for (out, index_last, reduced_shape, repeated), top in zip(both, tops):
+            shifted = last.tile(full, F32, bufs=2)
+            nc.vector.tensor_tensor(out=shifted[:], in0=by_row, in1=repeated(top[:]), op=ALU.subtract)
+            nc.scalar.activation(out=shifted[:], in_=shifted[:], func=ACT.Exp)
+            shifteds.append(shifted)
+        for (out, index_last, reduced_shape, repeated), shifted in zip(both, shifteds):
+            total = last.tile(reduced_shape, F32, bufs=2)
+            nc.vector.tensor_reduce(out=total[:], in_=index_last(shifted[:]), axis=AXIS.X, op=ALU.add)
+            nc.vector.reciprocal(out=total[:], in_=total[:])
+            totals.append(total)
+        for (out, index_last, reduced_shape, repeated), shifted, total in zip(both, shifteds, totals):
+            weights = last.tile([P, B, TOKENS, SLOTS], F32, bufs=2)
+            nc.vector.tensor_tensor(
+                out=weights[:],
+                in0=shifted[:].rearrange("r slot s b -> r b s slot"),
+                in1=repeated(total[:]).rearrange("r slot s b -> r b s slot"),
+                op=ALU.mult,
+            )
+            nc.sync.dma_start(
+                out=out.rearrange("x g k s slot -> (x g k) (s slot)").rearrange("(b r) w -> r b w", r=P),
+                in_=weights[:].rearrange("r b s slot -> r b (s slot)"),
+            )

@@ -15,23 +15,22 @@ AXIS = mybir.AxisListType
 P = 128
 PACK = 4
 EXPERTS = 8
-GROUPS = 256
-HALVES = GROUPS // P
+HALVES = 2
+STEPS = EXPERTS * HALVES
 TOKENS = 8
 SEGMENTS = 2
+UNITS = STEPS * SEGMENTS
 INNER = 2
 SLOTS = INNER * SEGMENTS
 D = 512
 WORDS = D // 2
-T = 16
-B = GROUPS // T
-LO = B // HALVES
-BANK = 512
-PAIRS = HALVES * SEGMENTS * INNER
-PER_BANK = BANK // P
+T = 8
+B = 16
+QUAD = 32
+QUAD_GROUPS = QUAD // TOKENS
 EPS = 1e-6
 
-FLOPS = 2 * EXPERTS * GROUPS * SEGMENTS * D * INNER * D + 2 * EXPERTS * GROUPS * TOKENS * SLOTS * D
+FLOPS = 2 * STEPS * P * SEGMENTS * D * INNER * D + 2 * STEPS * P * TOKENS * SLOTS * D
 
 
 def tile_hierarchicalsoftmoe2dblock_pb_t_kernel(tc, yn, means, w_slot2, out_0, out_1):
@@ -41,403 +40,354 @@ def tile_hierarchicalsoftmoe2dblock_pb_t_kernel(tc, yn, means, w_slot2, out_0, o
 
     with ExitStack() as ctx:
         consts = ctx.enter_context(tc.tile_pool(name="consts", bufs=1))
-        first_in = ctx.enter_context(tc.tile_pool(name="first_in", bufs=2))
-        token_in = ctx.enter_context(tc.tile_pool(name="token_in", bufs=2 * HALVES))
-        grouped = ctx.enter_context(tc.tile_pool(name="grouped", bufs=2))
-        packed_first = ctx.enter_context(tc.tile_pool(name="packed_first", bufs=3))
-        packed_second = ctx.enter_context(tc.tile_pool(name="packed_second", bufs=2))
-        norms = ctx.enter_context(tc.tile_pool(name="norms", bufs=2))
-        unread = ctx.enter_context(tc.tile_pool(name="unread", bufs=4))
-        picked = ctx.enter_context(tc.tile_pool(name="picked", bufs=2))
-        last = ctx.enter_context(tc.tile_pool(name="last", bufs=1))
-        turned_ps = ctx.enter_context(tc.psum_pool(name="turned_ps", bufs=2))
-        rows_ps = ctx.enter_context(tc.psum_pool(name="rows_ps", bufs=2))
-        cols_ps = ctx.enter_context(tc.psum_pool(name="cols_ps", bufs=2))
-        spread_ps = ctx.enter_context(tc.psum_pool(name="spread_ps", bufs=1))
+        w_pool = ctx.enter_context(tc.tile_pool(name="w_pool", bufs=3))
+        m_pool = ctx.enter_context(tc.tile_pool(name="m_pool", bufs=4))
+        y_pool = ctx.enter_context(tc.tile_pool(name="y_pool", bufs=4))
+        two = ctx.enter_context(tc.tile_pool(name="two", bufs=2))
+        three = ctx.enter_context(tc.tile_pool(name="three", bufs=3))
+        small = ctx.enter_context(tc.tile_pool(name="small", bufs=4))
+        last = ctx.enter_context(tc.tile_pool(name="last", bufs=2))
+        turned_ps = ctx.enter_context(tc.psum_pool(name="turned_ps", bufs=3))
+        rows_ps = ctx.enter_context(tc.psum_pool(name="rows_ps", bufs=4))
         logit_ps = ctx.enter_context(tc.psum_pool(name="logit_ps", bufs=1))
         ctx.enter_context(tc.manual_schedule())
 
-        ident = consts.tile([P, P], F32)
-        make_identity(nc, ident[:])
-        by_t = consts.tile([P, P], F32)
-        nc.vector.tensor_copy(
-            out=by_t[:].rearrange("i (t lo) -> i t lo", t=T),
-            in_=ident[:].rearrange("i (lo t) -> i t lo", t=T),
-        )
-        own_group = consts.tile([P, B], F32)
-        nc.vector.tensor_reduce(
-            out=own_group[:], in_=ident[:].rearrange("q (s b) -> q b s", b=B), axis=AXIS.X, op=ALU.add
-        )
-        logits = consts.tile([P, SLOTS, T * EXPERTS], F32)
-
         w_raw, m_raw, y_raw = {}, {}, {}
-        m_grouped, w_grouped, y_grouped, s_grouped = {}, {}, {}, {}
-        w_codes, w_scales, m_codes, m_scales = {}, {}, {}, {}
-        y_codes, y_scales, s_codes, s_scales = {}, {}, {}, {}
-        square_sums, link, inv_norm_all = {}, {}, {}
+        w_grouped, w_codes, w_scales = {}, {}, {}
+        m_grouped, m_codes, m_scales = {}, {}, {}
+        y_grouped, y_codes, y_scales = {}, {}, {}
+        s_grouped, s_codes, s_scales = {}, {}, {}
+        se_banks, square_sums, inv_norms, se2_rows = {}, {}, {}, {}
 
-        def exists(k):
-            return 0 <= k < EXPERTS
-
-        def load_first(k):
-            if not exists(k):
+        def load_w(k, pieces):
+            if not 0 <= k < EXPERTS:
                 return
-            w_in = first_in.tile([P, PACK, INNER * D], BF16)
-            nc.sync.dma_start(out=w_in[:], in_=w_slot2[k].rearrange("(p j) c -> p j c", j=PACK))
-            m_in = first_in.tile([P, HALVES, SEGMENTS * D], BF16)
-            nc.sync.dma_start(out=m_in[:], in_=means_rows[k].rearrange("(h p) x -> p h x", p=P))
-            m_raw[k], w_raw[k] = m_in, w_in
+            w_in = w_pool.tile([P, PACK, INNER * D], BF16)
+            width = INNER * D // pieces
+            for i in range(pieces):
+                cols = slice(i * width, (i + 1) * width)
+                nc.sync.dma_start(
+                    out=w_in[:, :, cols], in_=w_slot2[k].rearrange("(p j) c -> p j c", j=PACK)[:, :, cols]
+                )
+            w_raw[k] = w_in
 
-        def load_tokens(k):
-            if not exists(k):
+        def load_means(n):
+            if not 0 <= n < STEPS:
                 return
-            y_raw[k] = []
-            for half in range(HALVES):
-                y_in = token_in.tile([P, TOKENS * D], BF16)
-                nc.sync.dma_start(out=y_in[:], in_=yn_rows[k, half * P : (half + 1) * P, :])
-                y_raw[k].append(y_in)
+            k, h = divmod(n, HALVES)
+            m_in = m_pool.tile([P, SEGMENTS * D], BF16)
+            nc.sync.dma_start(out=m_in[:], in_=means_rows[k, h * P : (h + 1) * P, :])
+            m_raw[n] = m_in
 
-        def copy_turned(filling, out, in_):
-            if filling:
-                nc.vector.tensor_copy(out=out, in_=in_)
+        def load_tokens(n):
+            if not 0 <= n < STEPS:
+                return
+            k, h = divmod(n, HALVES)
+            y_in = y_pool.tile([P, TOKENS * D], BF16)
+            nc.sync.dma_start(out=y_in[:], in_=yn_rows[k, h * P : (h + 1) * P, :])
+            y_raw[n] = y_in
+
+        def regroup_w(k, i, on_scalar):
+            if not 0 <= k < EXPERTS:
+                return
+            e, part = divmod(i, 2)
+            if part == 0:
+                w_new = three.tile([P, D * PACK], BF16, align_bytes=64, name="w_grouped")
+                w_grouped[k, e] = w_new
+            width = D // 2
+            dst = w_grouped[k, e][:].rearrange("p (c j) -> p c j", j=PACK)[:, part * width : (part + 1) * width, :]
+            src = w_raw[k][:].rearrange("p j c -> p c j")[:, i * width : (i + 1) * width, :]
+            if on_scalar:
+                nc.scalar.copy(out=dst, in_=src)
             else:
-                nc.scalar.copy(out=out, in_=in_)
+                nc.vector.tensor_copy(out=dst, in_=src)
 
-        def turn_means(k, half, filling):
-            if not exists(k):
+        def quantise_w(k, e):
+            if not 0 <= k < EXPERTS:
                 return
-            if half == 0:
-                m_new = grouped.tile([P, HALVES * SEGMENTS * P * PACK], BF16, align_bytes=64, name="m_grouped")
-                m_grouped[k] = m_new
-            m_pairs = m_grouped[k][:].bitcast(F32).rearrange("p (g c u) -> p g c u", c=P, u=2)
-            m_words = m_raw[k][:].bitcast(F32)
+            codes = two.tile([P, D], U32, align_bytes=64, name="w_codes%d" % e)
+            scales = two.tile([P, D], U8, align_bytes=64, name="w_scales%d" % e)
+            nc.vector.quantize_mx(out=codes[:].bitcast(FP8X4), scales=scales[:], in_=w_grouped[k, e][:])
+            w_codes[k, e], w_scales[k, e] = codes, scales
+
+        def turn_means(n):
+            if not 0 <= n < STEPS:
+                return
+            words = m_raw[n][:].bitcast(F32)
             turned = turned_ps.tile([P, SEGMENTS, 2, P], F32)
             for m in range(SEGMENTS):
                 for u in range(2):
-                    every_second = slice(m * WORDS + u, (m + 1) * WORDS, 2)
-                    nc.tensor.transpose(turned[:, m, u, :], m_words[:, half, every_second], by_t[:])
-            copy_turned(
-                filling,
-                out=m_pairs[:, SEGMENTS * half : SEGMENTS * (half + 1), :, :],
+                    nc.tensor.transpose(
+                        turned[:, m, u, :], words[:, m * WORDS + u : (m + 1) * WORDS : 2], ident[:]
+                    )
+            m_new = two.tile([P, SEGMENTS * P * PACK], BF16, align_bytes=64, name="m_grouped")
+            nc.scalar.copy(
+                out=m_new[:].bitcast(F32).rearrange("p (m c u) -> p m c u", c=P, u=2),
                 in_=turned[:].rearrange("p m u c -> p m c u"),
             )
+            m_grouped[n] = m_new
 
-        def quantise_means(k):
-            if not exists(k):
+        def quantise_means(n):
+            if not 0 <= n < STEPS:
                 return
-            codes = packed_first.tile([P, HALVES * SEGMENTS * P], U32, align_bytes=64, name="m_codes")
-            scales = packed_first.tile([P, HALVES * SEGMENTS * P], U8, align_bytes=64, name="m_scales")
-            nc.vector.quantize_mx(out=codes[:].bitcast(FP8X4), scales=scales[:], in_=m_grouped[k][:])
-            m_codes[k], m_scales[k] = codes, scales
+            codes = three.tile([P, SEGMENTS * P], U32, align_bytes=64, name="m_codes")
+            scales = three.tile([P, SEGMENTS * P], U8, align_bytes=64, name="m_scales")
+            nc.vector.quantize_mx(out=codes[:].bitcast(FP8X4), scales=scales[:], in_=m_grouped[n][:])
+            m_codes[n], m_scales[n] = codes, scales
 
-        def regroup_w(k, a):
-            if not exists(k):
+        def turn_tokens(n, i):
+            if not 0 <= n < STEPS:
                 return
-            if a == 0:
-                w_new = grouped.tile([P, INNER * D * PACK], BF16, align_bytes=64, name="w_grouped")
-                w_grouped[k] = w_new
-            dst = w_grouped[k][:].rearrange("p (a odd q j) -> p a q odd j", a=2 * INNER, odd=2, j=PACK)
-            src = w_raw[k][:].rearrange("p j (e q u odd) -> p e u q odd j", e=INNER, u=2, odd=2)
-            if a % 2 == 0:
-                nc.vector.tensor_copy(out=dst[:, a], in_=src[:, a // 2, a % 2])
-            else:
-                nc.scalar.copy(out=dst[:, a], in_=src[:, a // 2, a % 2])
-
-        def quantise_w(k, e):
-            if not exists(k):
-                return
-            if e == 0:
-                codes = packed_first.tile([P, INNER * D], U32, align_bytes=64, name="w_codes")
-                scales = packed_first.tile([P, INNER * D], U8, align_bytes=64, name="w_scales")
-                w_codes[k], w_scales[k] = codes, scales
-            nc.vector.quantize_mx(
-                out=w_codes[k][:, e * D : (e + 1) * D].bitcast(FP8X4),
-                scales=w_scales[k][:, e * D : (e + 1) * D],
-                in_=w_grouped[k][:, e * D * PACK : (e + 1) * D * PACK],
-            )
-
-        def turn_tokens(k, i, filling):
-            if not exists(k):
-                return
-            half, s0 = i // (TOKENS // 2), 2 * (i % (TOKENS // 2))
             if i == 0:
-                y_new = grouped.tile([P, T * TOKENS * B * PACK], BF16, align_bytes=64, name="y_grouped")
-                y_grouped[k] = y_new
-            y_pairs = y_grouped[k][:].bitcast(F32).rearrange("p (t s b u) -> p s t b u", t=T, s=TOKENS, u=2)
-            y_words = y_raw[k][half][:].bitcast(F32)
+                y_new = two.tile([P, P * TOKENS * PACK], BF16, align_bytes=64, name="y_grouped")
+                y_grouped[n] = y_new
+            words = y_raw[n][:].bitcast(F32)
             turned = turned_ps.tile([P, 2, 2, P], F32)
             for s in range(2):
                 for u in range(2):
-                    every_second = slice((s0 + s) * WORDS + u, (s0 + s + 1) * WORDS, 2)
-                    nc.tensor.transpose(turned[:, s, u, :], y_words[:, every_second], by_t[:])
-            copy_turned(
-                filling,
-                out=y_pairs[:, s0 : s0 + 2, :, LO * half : LO * (half + 1), :],
-                in_=turned[:].rearrange("p s u (t lo) -> p s t lo u", t=T),
-            )
+                    row = 2 * i + s
+                    nc.tensor.transpose(turned[:, s, u, :], words[:, row * WORDS + u : (row + 1) * WORDS : 2], ident[:])
+            pairs = y_grouped[n][:].bitcast(F32).rearrange("p (g s u) -> p g s u", s=TOKENS, u=2)
+            nc.scalar.copy(out=pairs[:, :, 2 * i : 2 * i + 2, :], in_=turned[:].rearrange("p s u g -> p g s u"))
 
-        def quantise_tokens(k, part):
-            if not exists(k):
+        def quantise_tokens(n, part):
+            if not 0 <= n < STEPS:
                 return
             if part == 0:
-                codes = packed_second.tile([P, T * P], U32, align_bytes=64, name="y_codes")
-                scales = packed_second.tile([P, T * P], U8, align_bytes=64, name="y_scales")
-                y_codes[k], y_scales[k] = codes, scales
+                codes = three.tile([P, T * P], U32, align_bytes=64, name="y_codes")
+                scales = three.tile([P, T * P], U8, align_bytes=64, name="y_scales")
+                y_codes[n], y_scales[n] = codes, scales
             width = T * P // 2
             nc.vector.quantize_mx(
-                out=y_codes[k][:, part * width : (part + 1) * width].bitcast(FP8X4),
-                scales=y_scales[k][:, part * width : (part + 1) * width],
-                in_=y_grouped[k][:, part * width * PACK : (part + 1) * width * PACK],
+                out=y_codes[n][:, part * width : (part + 1) * width].bitcast(FP8X4),
+                scales=y_scales[n][:, part * width : (part + 1) * width],
+                in_=y_grouped[n][:, part * width * PACK : (part + 1) * width * PACK],
             )
 
-        def sum_squares(k, i):
-            if not exists(k):
+        def multiply_means(unit):
+            if not 0 <= unit < UNITS:
                 return
-            e, g = i // PER_BANK, i % PER_BANK
-            if i == 0:
-                sums = norms.tile([P, PAIRS], F32)
-                square_sums[k] = sums
-            se_rows = rows_ps.tile([P, D], F32)
-            nc.tensor.matmul_mx(
-                out=se_rows[:],
-                lhsT=m_codes[k][:, g * P : (g + 1) * P].bitcast(FP8X4),
-                lhsT_scale=m_scales[k][:, g * P : (g + 1) * P],
-                rhs=w_codes[k][:, e * D : (e + 1) * D].bitcast(FP8X4),
-                rhs_scale=w_scales[k][:, e * D : (e + 1) * D],
-                start=True,
-                stop=True,
-            )
-            squares = unread.tile([P, D], BF16)
-            nc.scalar.activation(
-                out=squares[:], in_=se_rows[:], func=ACT.Square, accum_out=square_sums[k][:, i : i + 1]
-            )
-
-        def mean_squares(k, part):
-            if not exists(k):
-                return
-            mean_sq = norms.tile([P, PER_BANK], F32)
-            nc.vector.tensor_scalar(
-                out=mean_sq[:],
-                in0=square_sums[k][:, part * PER_BANK : (part + 1) * PER_BANK],
-                scalar1=EPS,
-                scalar2=1.0 / D,
-                op0=ALU.add,
-                op1=ALU.mult,
-            )
-            link[k, part] = mean_sq
-
-        def roots(k, part):
-            if not exists(k):
-                return
-            rms = norms.tile([P, PER_BANK], F32)
-            nc.scalar.sqrt(out=rms[:], in_=link[k, part][:])
-            link[k, part] = rms
-
-        def inverses(k, part):
-            if not exists(k):
-                return
-            inv_norm = norms.tile([P, PER_BANK], F32)
-            nc.vector.reciprocal(out=inv_norm[:], in_=link[k, part][:])
-            link[k, part] = inv_norm
-
-        def spread_norms(k, part):
-            if not exists(k):
-                return
-            if part == 0:
-                everywhere = norms.tile([P, PAIRS, P], F32)
-                inv_norm_all[k] = everywhere
-            spread = spread_ps.tile([P, PER_BANK, P], F32)
-            for i in range(PER_BANK):
-                nc.tensor.transpose(spread[:, i, :], link[k, part][:, i : i + 1].to_broadcast([P, P]), ident[:])
-            nc.scalar.copy(out=inv_norm_all[k][:, part * PER_BANK : (part + 1) * PER_BANK, :], in_=spread[:])
-
-        def make_slots(k, i):
-            if not exists(k):
-                return
-            e, g = i // PER_BANK, i % PER_BANK
-            half, m = g // SEGMENTS, g % SEGMENTS
-            if i == 0:
-                s_new = grouped.tile([P, T * SLOTS * B * PACK], BF16, align_bytes=64, name="s_grouped")
-                s_grouped[k] = s_new
-            se_cols = cols_ps.tile([P, PACK, P], F32)
-            for j in range(PACK):
-                chunk = slice((PACK * e + j) * P, (PACK * e + j + 1) * P)
+            n, m = divmod(unit, SEGMENTS)
+            k = n // HALVES
+            for e in range(INNER):
+                se = rows_ps.tile([P, D], F32)
                 nc.tensor.matmul_mx(
-                    out=se_cols[:, j, :],
-                    lhsT=w_codes[k][:, chunk].bitcast(FP8X4),
-                    lhsT_scale=w_scales[k][:, chunk],
-                    rhs=m_codes[k][:, g * P : (g + 1) * P].bitcast(FP8X4),
-                    rhs_scale=m_scales[k][:, g * P : (g + 1) * P],
+                    out=se[:],
+                    lhsT=m_codes[n][:, m * P : (m + 1) * P].bitcast(FP8X4),
+                    lhsT_scale=m_scales[n][:, m * P : (m + 1) * P],
+                    rhs=w_codes[k, e][:].bitcast(FP8X4),
+                    rhs_scale=w_scales[k, e][:],
                     start=True,
                     stop=True,
                 )
-            by_column = s_grouped[k][:].rearrange("p (t slot b j) -> p slot t b j", t=T, slot=SLOTS, j=PACK)
-            scale = inv_norm_all[k][:, i, :].rearrange("p (t lo) -> p t lo", t=T)
-            nc.vector.tensor_tensor(
-                out=by_column[:, SEGMENTS * e + m, :, LO * half : LO * (half + 1), :],
-                in0=se_cols[:].rearrange("p j (t lo) -> p t lo j", t=T),
-                in1=scale.unsqueeze(3).to_broadcast([P, T, LO, PACK]),
-                op=ALU.mult,
+                se_banks[unit, e] = se
+
+        def sum_squares(unit, e):
+            if not 0 <= unit < UNITS:
+                return
+            if e == 0:
+                sums = small.tile([P, INNER], F32)
+                square_sums[unit] = sums
+            squares = small.tile([P, D], BF16)
+            nc.scalar.activation(
+                out=squares[:], in_=se_banks[unit, e][:], func=ACT.Square, accum_out=square_sums[unit][:, e : e + 1]
             )
 
-        def quantise_slots(k, part):
-            if not exists(k):
+        def invert_norms(unit):
+            if not 0 <= unit < UNITS:
                 return
-            if part == 0:
-                codes = packed_second.tile([P, T * SLOTS * B], U32, align_bytes=64, name="s_codes")
-                scales = packed_second.tile([P, T * SLOTS * B], U8, align_bytes=64, name="s_scales")
-                s_codes[k], s_scales[k] = codes, scales
-            width = T * SLOTS * B // 2
-            nc.vector.quantize_mx(
-                out=s_codes[k][:, part * width : (part + 1) * width].bitcast(FP8X4),
-                scales=s_scales[k][:, part * width : (part + 1) * width],
-                in_=s_grouped[k][:, part * width * PACK : (part + 1) * width * PACK],
+            mean_sq = small.tile([P, INNER], F32)
+            nc.gpsimd.tensor_scalar(
+                out=mean_sq[:], in0=square_sums[unit][:], scalar1=EPS, scalar2=1.0 / D, op0=ALU.add, op1=ALU.mult
             )
+            inv_norm = small.tile([P, INNER], F32)
+            nc.gpsimd.tensor_tensor(out=inv_norm[:], in0=mean_sq[:], in1=minus_half[:], op=ALU.pow)
+            inv_norms[unit] = inv_norm
 
-        def cross(k, part):
-            if not exists(k):
+        def normalise(unit, e, on_scalar):
+            if not 0 <= unit < UNITS:
                 return
-            t0 = part * T // 2
-            crossed = logit_ps.tile([P, T // 2, SLOTS * B], F32)
-            for i in range(T // 2):
-                t = t0 + i
+            if e == 0:
+                rows = two.tile([P, INNER * D], BF16, name="se2_rows")
+                se2_rows[unit] = rows
+            out = se2_rows[unit][:, e * D : (e + 1) * D].rearrange("p (u q o) -> p u q o", u=2, o=2)
+            in_ = se_banks[unit, e][:].rearrange("p (q u o) -> p u q o", u=2, o=2)
+            if on_scalar:
+                nc.scalar.activation(out=out, in_=in_, func=ACT.Copy, scale=inv_norms[unit][:, e : e + 1])
+            else:
+                nc.vector.tensor_scalar(
+                    out=out, in0=in_, scalar1=inv_norms[unit][:, e : e + 1], scalar2=None, op0=ALU.mult
+                )
+
+        def turn_slots(unit):
+            if not 0 <= unit < UNITS:
+                return
+            n, m = divmod(unit, SEGMENTS)
+            if m == 0:
+                s_new = two.tile([P, P * SLOTS * PACK], BF16, align_bytes=64, name="s_grouped")
+                s_grouped[n] = s_new
+            words = se2_rows[unit][:].bitcast(F32)
+            turned = turned_ps.tile([P, INNER, 2, P], F32)
+            for e in range(INNER):
+                for u in range(2):
+                    first = e * WORDS + u * P
+                    nc.tensor.transpose(turned[:, e, u, :], words[:, first : first + P], ident[:])
+            pairs = s_grouped[n][:].bitcast(F32).rearrange("p (g m e u) -> p m g e u", m=SEGMENTS, e=INNER, u=2)
+            nc.scalar.copy(out=pairs[:, m], in_=turned[:].rearrange("p e u g -> p g e u"))
+
+        def quantise_slots(n):
+            if not 0 <= n < STEPS:
+                return
+            codes = two.tile([P, P * SLOTS], U32, align_bytes=64, name="s_codes")
+            scales = two.tile([P, P * SLOTS], U8, align_bytes=64, name="s_scales")
+            nc.vector.quantize_mx(out=codes[:].bitcast(FP8X4), scales=scales[:], in_=s_grouped[n][:])
+            s_codes[n], s_scales[n] = codes, scales
+
+        def cross(n):
+            if not 0 <= n < STEPS:
+                return
+            crossed = logit_ps.tile([P, T, B, SLOTS], F32)
+            for t in range(T):
                 nc.tensor.matmul_mx(
-                    out=crossed[:, i, :],
-                    lhsT=y_codes[k][:, t * P : (t + 1) * P].bitcast(FP8X4),
-                    lhsT_scale=y_scales[k][:, t * P : (t + 1) * P],
-                    rhs=s_codes[k][:, t * SLOTS * B : (t + 1) * SLOTS * B].bitcast(FP8X4),
-                    rhs_scale=s_scales[k][:, t * SLOTS * B : (t + 1) * SLOTS * B],
+                    out=crossed[:, t].rearrange("q b x -> q (b x)"),
+                    lhsT=y_codes[n][:, t * P : (t + 1) * P].bitcast(FP8X4),
+                    lhsT_scale=y_scales[n][:, t * P : (t + 1) * P],
+                    rhs=s_codes[n][:, t * B * SLOTS : (t + 1) * B * SLOTS].bitcast(FP8X4),
+                    rhs_scale=s_scales[n][:, t * B * SLOTS : (t + 1) * B * SLOTS],
                     start=True,
                     stop=True,
                 )
             return crossed
 
-        def pick(k, part, crossed):
-            if not exists(k):
+        def pick(n, crossed):
+            if not 0 <= n < STEPS:
                 return
-            t0 = part * T // 2
-            own = picked.tile([P, T // 2 * SLOTS, B], F32)
-            nc.vector.tensor_tensor(
-                out=own[:],
-                in0=crossed[:].rearrange("q t (slot b) -> q (t slot) b", b=B),
-                in1=own_group[:].unsqueeze(1).to_broadcast([P, T // 2 * SLOTS, B]),
-                op=ALU.mult,
-            )
+            own = two.tile([P, T, QUAD_GROUPS, SLOTS], F32)
+            for a in range(P // QUAD):
+                rows = slice(a * QUAD, (a + 1) * QUAD)
+                groups = slice(a * QUAD_GROUPS, (a + 1) * QUAD_GROUPS)
+                nc.vector.tensor_tensor(
+                    out=own[rows],
+                    in0=crossed[rows, :, groups, :],
+                    in1=own_group[rows].unsqueeze(1).unsqueeze(3).to_broadcast([QUAD, T, QUAD_GROUPS, SLOTS]),
+                    op=ALU.mult,
+                )
             nc.vector.tensor_reduce(
-                out=logits[:].rearrange("q slot (t k) -> q slot t k", k=EXPERTS)[:, :, t0 : t0 + T // 2, k],
-                in_=own[:].rearrange("q (t slot) b -> q slot t b", slot=SLOTS),
+                out=logits[:].rearrange("q (e m) r -> q r m e", m=SEGMENTS)[:, n * T : (n + 1) * T],
+                in_=own[:].rearrange("q t c (m e) -> q t m e c", e=INNER),
                 axis=AXIS.X,
                 op=ALU.add,
             )
 
-        load_first(0)
+        load_w(0, 2)
+        load_means(0)
         load_tokens(0)
-        load_first(1)
-        for k in range(-2, EXPERTS + 1):
-            filling = k < 0
+        load_means(1)
+        load_tokens(1)
+        load_w(1, 2)
+        load_means(2)
+        load_tokens(2)
+        load_means(3)
+        load_tokens(3)
+        load_w(2, 1)
 
-            make_slots(k, 0)
-            sum_squares(k + 1, 0)
-            turn_tokens(k + 1, 0, filling)
-            mean_squares(k, 1)
-            quantise_slots(k - 1, 0)
-            regroup_w(k + 2, 0)
+        ident = consts.tile([P, P], F32)
+        make_identity(nc, ident[:])
+        minus_half = consts.tile([P, INNER], F32)
+        nc.gpsimd.memset(minus_half[:], -0.5)
+        own_group = consts.tile([P, QUAD_GROUPS], F32)
+        nc.vector.tensor_reduce(
+            out=own_group[:],
+            in_=ident[:].rearrange("q (a c s) -> q c a s", c=QUAD_GROUPS, s=TOKENS),
+            axis=AXIS.XY,
+            op=ALU.add,
+        )
+        logits = consts.tile([P, SLOTS, STEPS * T], F32)
 
-            make_slots(k, 1)
-            sum_squares(k + 1, 1)
-            crossed = cross(k - 1, 0)
-            turn_tokens(k + 1, 1, filling)
-            roots(k, 1)
-            quantise_slots(k - 1, 1)
-            regroup_w(k + 2, 1)
+        for unit in range(-5, UNITS + 4):
+            n, m = divmod(unit, SEGMENTS)
+            filling = unit < 0
+            w_at = unit + 5
+            k_next, quarter = divmod(w_at, 4)
 
-            make_slots(k, 2)
-            sum_squares(k + 1, 2)
-            turn_tokens(k + 1, 2, filling)
-            inverses(k, 1)
-            quantise_tokens(k, 0)
-            regroup_w(k + 2, 2)
+            multiply_means(unit)
+            if m == 0:
+                crossed = cross(n - 2)
+            sum_squares(unit, 0)
+            sum_squares(unit, 1)
+            invert_norms(unit)
+            normalise(unit - 1, 0, False)
+            normalise(unit - 1, 1, m == 0)
+            if quarter == 2:
+                quantise_w(k_next, 0)
+            if quarter == 0:
+                quantise_w(k_next - 1, 1)
+            regroup_w(k_next, quarter, filling and quarter % 2 == 1)
+            turn_tokens(n + 1, 2 * m)
+            turn_slots(unit - 1)
+            quantise_tokens(n, m)
+            turn_tokens(n + 1, 2 * m + 1)
+            if m == 1:
+                quantise_slots(n - 1)
+                turn_means(n + 2)
+            else:
+                quantise_means(n + 1)
+                pick(n - 2, crossed)
 
-            make_slots(k, 3)
-            sum_squares(k + 1, 3)
-            turn_tokens(k + 1, 3, filling)
-            spread_norms(k, 1)
-            pick(k - 1, 0, crossed)
-            regroup_w(k + 2, 3)
-
-            make_slots(k, 4)
-            sum_squares(k + 1, 4)
-            crossed = cross(k - 1, 1)
-            turn_tokens(k + 1, 4, filling)
-            turn_means(k + 2, 0, filling)
-            mean_squares(k + 1, 0)
-            quantise_tokens(k, 1)
-
-            make_slots(k, 5)
-            sum_squares(k + 1, 5)
-            turn_tokens(k + 1, 5, filling)
-            turn_means(k + 2, 1, filling)
-            roots(k + 1, 0)
-            quantise_w(k + 2, 0)
-
-            make_slots(k, 6)
-            sum_squares(k + 1, 6)
-            turn_tokens(k + 1, 6, filling)
-            inverses(k + 1, 0)
-            pick(k - 1, 1, crossed)
-
-            make_slots(k, 7)
-            sum_squares(k + 1, 7)
-            turn_tokens(k + 1, 7, filling)
-            spread_norms(k + 1, 0)
-            quantise_means(k + 2)
-            quantise_w(k + 2, 1)
-
-            load_tokens(k + 3)
-            load_first(k + 4)
+            if m == 1 and n >= -2:
+                load_means(n + 6)
+            if m == 1 and n >= -1:
+                load_tokens(n + 5)
+            if quarter == 3:
+                load_w(k_next + 3, 1)
 
         by_row_ps = logit_ps.tile([P, SLOTS, P], F32, tag="crossed")
         for slot in range(SLOTS):
             nc.tensor.transpose(by_row_ps[:, slot, :], logits[:, slot, :], ident[:])
-        by_row = by_row_ps[:].rearrange("r slot (s b) -> r slot s b", b=B)
-        full = [P, SLOTS, TOKENS, B]
+        by_row = by_row_ps[:].rearrange("r slot (b s) -> r slot b s", b=B)
+        full = [P, SLOTS, B, TOKENS]
         over_tokens = (
             out_0,
-            lambda x: x.rearrange("r slot s b -> r slot b s"),
+            nc.sync,
+            lambda x: x,
             [P, SLOTS, B],
-            lambda x: x.unsqueeze(2).to_broadcast(full),
+            lambda x: x.unsqueeze(3).to_broadcast(full),
         )
         over_slots = (
             out_1,
-            lambda x: x.rearrange("r slot s b -> r s b slot"),
-            [P, TOKENS, B],
+            nc.scalar,
+            lambda x: x.rearrange("r slot b s -> r b s slot"),
+            [P, B, TOKENS],
             lambda x: x.unsqueeze(1).to_broadcast(full),
         )
         both = (over_tokens, over_slots)
         tops, shifteds, totals = [], [], []
-        for out, index_last, reduced_shape, repeated in both:
-            top = last.tile(reduced_shape, F32, bufs=2)
+        for out, queue, index_last, reduced_shape, repeated in both:
+            top = last.tile(reduced_shape, F32)
             nc.vector.tensor_reduce(out=top[:], in_=index_last(by_row), axis=AXIS.X, op=ALU.max)
             tops.append(top)
-        for (out, index_last, reduced_shape, repeated), top in zip(both, tops):
-            shifted = last.tile(full, F32, bufs=2)
+        for (out, queue, index_last, reduced_shape, repeated), top in zip(both, tops):
+            shifted = last.tile(full, F32)
             nc.vector.tensor_tensor(out=shifted[:], in0=by_row, in1=repeated(top[:]), op=ALU.subtract)
             nc.scalar.activation(out=shifted[:], in_=shifted[:], func=ACT.Exp)
             shifteds.append(shifted)
-        for (out, index_last, reduced_shape, repeated), shifted in zip(both, shifteds):
-            total = last.tile(reduced_shape, F32, bufs=2)
+        for (out, queue, index_last, reduced_shape, repeated), shifted in zip(both, shifteds):
+            total = last.tile(reduced_shape, F32)
             nc.vector.tensor_reduce(out=total[:], in_=index_last(shifted[:]), axis=AXIS.X, op=ALU.add)
             nc.vector.reciprocal(out=total[:], in_=total[:])
             totals.append(total)
-        for (out, index_last, reduced_shape, repeated), shifted, total in zip(both, shifteds, totals):
-            weights = last.tile([P, B, TOKENS, SLOTS], F32, bufs=2)
+        for (out, queue, index_last, reduced_shape, repeated), shifted, total in zip(both, shifteds, totals):
+            weights = last.tile([P, B, TOKENS, SLOTS], F32)
             nc.vector.tensor_tensor(
                 out=weights[:],
-                in0=shifted[:].rearrange("r slot s b -> r b s slot"),
-                in1=repeated(total[:]).rearrange("r slot s b -> r b s slot"),
+                in0=shifted[:].rearrange("r slot b s -> r b s slot"),
+                in1=repeated(total[:]).rearrange("r slot b s -> r b s slot"),
                 op=ALU.mult,
             )
-            nc.sync.dma_start(
-                out=out.rearrange("x g k s slot -> (x g k) (s slot)").rearrange("(b r) w -> r b w", r=P),
-                in_=weights[:].rearrange("r b s slot -> r b (s slot)"),
-            )
+            per_expert = out.rearrange("x g k s slot -> k (x g) (s slot)")
+            rows = HALVES * T
+            for k in range(EXPERTS):
+                queue.dma_start(
+                    out=per_expert[k].rearrange("(r b) w -> r b w", b=B),
+                    in_=weights[k * rows : (k + 1) * rows].rearrange("r b s slot -> r b (s slot)"),
+                )

@@ -196,12 +196,14 @@ def tile_hierarchicalsoftmoe2dblock_pb_t_kernel(tc, yn, means, w_slot2, out_0, o
         def invert_norms(unit):
             if not 0 <= unit < UNITS:
                 return
-            mean_sq = small.tile([P, INNER], F32)
-            nc.gpsimd.tensor_scalar(
-                out=mean_sq[:], in0=square_sums[unit][:], scalar1=EPS, scalar2=1.0 / D, op0=ALU.add, op1=ALU.mult
-            )
             inv_norm = small.tile([P, INNER], F32)
-            nc.gpsimd.tensor_tensor(out=inv_norm[:], in0=mean_sq[:], in1=minus_half[:], op=ALU.pow)
+            nc.scalar.activation(
+                out=inv_norm[:],
+                in_=square_sums[unit][:],
+                func=ACT.Abs_reciprocal_sqrt,
+                scale=1.0 / D,
+                bias=EPS / D,
+            )
             inv_norms[unit] = inv_norm
 
         def normalise(unit, e, on_scalar):
@@ -293,8 +295,6 @@ def tile_hierarchicalsoftmoe2dblock_pb_t_kernel(tc, yn, means, w_slot2, out_0, o
 
         ident = consts.tile([P, P], F32)
         make_identity(nc, ident[:])
-        minus_half = consts.tile([P, INNER], F32)
-        nc.gpsimd.memset(minus_half[:], -0.5)
         own_group = consts.tile([P, QUAD_GROUPS], F32)
         nc.vector.tensor_reduce(
             out=own_group[:],
@@ -310,29 +310,28 @@ def tile_hierarchicalsoftmoe2dblock_pb_t_kernel(tc, yn, means, w_slot2, out_0, o
             w_at = unit + 5
             k_next, quarter = divmod(w_at, 4)
 
+            turn_tokens(n + 1, 2 * m)
+            turn_slots(unit - 2)
             multiply_means(unit)
-            if m == 0:
-                crossed = cross(n - 2)
             sum_squares(unit, 0)
             sum_squares(unit, 1)
             invert_norms(unit)
-            normalise(unit - 1, 0, False)
-            normalise(unit - 1, 1, m == 0)
             if quarter == 2:
                 quantise_w(k_next, 0)
             if quarter == 0:
                 quantise_w(k_next - 1, 1)
             regroup_w(k_next, quarter, filling and quarter % 2 == 1)
-            turn_tokens(n + 1, 2 * m)
-            turn_slots(unit - 1)
             quantise_tokens(n, m)
+            normalise(unit - 1, 0, False)
+            normalise(unit - 1, 1, m == 0)
             turn_tokens(n + 1, 2 * m + 1)
             if m == 1:
-                quantise_slots(n - 1)
+                crossed = cross(n - 2)
                 turn_means(n + 2)
+                pick(n - 2, crossed)
             else:
                 quantise_means(n + 1)
-                pick(n - 2, crossed)
+                quantise_slots(n - 2)
 
             if m == 1 and n >= -2:
                 load_means(n + 6)

@@ -28,6 +28,7 @@ T = 8
 B = 16
 QUAD = 32
 QUAD_GROUPS = QUAD // TOKENS
+CROSS_COLUMNS = 256
 EPS = 1e-6
 
 FLOPS = 2 * STEPS * P * SEGMENTS * D * INNER * D + 2 * STEPS * P * TOKENS * SLOTS * D
@@ -57,7 +58,7 @@ def tile_hierarchicalsoftmoe2dblock_pb_t_kernel(tc, yn, means, w_slot2, out_0, o
         m_grouped, m_codes, m_scales = {}, {}, {}
         y_grouped, y_codes, y_scales = {}, {}, {}
         s_grouped, s_codes, s_scales = {}, {}, {}
-        se_banks, square_sums, inv_norms, se2_rows = {}, {}, {}, {}
+        se_banks, square_sums, inv_norms, se2_rows, crossed = {}, {}, {}, {}, {}
 
         def load_w(k, pieces):
             if not 0 <= k < EXPERTS:
@@ -164,23 +165,22 @@ def tile_hierarchicalsoftmoe2dblock_pb_t_kernel(tc, yn, means, w_slot2, out_0, o
                 in_=y_grouped[n][:, part * width * PACK : (part + 1) * width * PACK],
             )
 
-        def multiply_means(unit):
+        def multiply_means(unit, e):
             if not 0 <= unit < UNITS:
                 return
             n, m = divmod(unit, SEGMENTS)
             k = n // HALVES
-            for e in range(INNER):
-                se = rows_ps.tile([P, D], F32)
-                nc.tensor.matmul_mx(
-                    out=se[:],
-                    lhsT=m_codes[n][:, m * P : (m + 1) * P].bitcast(FP8X4),
-                    lhsT_scale=m_scales[n][:, m * P : (m + 1) * P],
-                    rhs=w_codes[k, e][:].bitcast(FP8X4),
-                    rhs_scale=w_scales[k, e][:],
-                    start=True,
-                    stop=True,
-                )
-                se_banks[unit, e] = se
+            se = rows_ps.tile([P, D], F32)
+            nc.tensor.matmul_mx(
+                out=se[:],
+                lhsT=m_codes[n][:, m * P : (m + 1) * P].bitcast(FP8X4),
+                lhsT_scale=m_scales[n][:, m * P : (m + 1) * P],
+                rhs=w_codes[k, e][:].bitcast(FP8X4),
+                rhs_scale=w_scales[k, e][:],
+                start=True,
+                stop=True,
+            )
+            se_banks[unit, e] = se
 
         def sum_squares(unit, e):
             if not 0 <= unit < UNITS:
@@ -245,32 +245,39 @@ def tile_hierarchicalsoftmoe2dblock_pb_t_kernel(tc, yn, means, w_slot2, out_0, o
             nc.vector.quantize_mx(out=codes[:].bitcast(FP8X4), scales=scales[:], in_=s_grouped[n][:])
             s_codes[n], s_scales[n] = codes, scales
 
-        def cross(n):
+        def cross(n, part):
             if not 0 <= n < STEPS:
                 return
-            crossed = logit_ps.tile([P, T, B, SLOTS], F32)
-            for t in range(T):
+            if part == 0:
+                crossed_new = logit_ps.tile([P, T * B * SLOTS], F32, name="crossed")
+                crossed[n] = crossed_new
+            for t in range(2 * part, 2 * part + 2):
+                first = t * B * SLOTS
+                width = B * SLOTS
+                while width < CROSS_COLUMNS and first + 2 * width <= T * B * SLOTS:
+                    width *= 2
+                cols = slice(first, first + width)
                 nc.tensor.matmul_mx(
-                    out=crossed[:, t].rearrange("q b x -> q (b x)"),
+                    out=crossed[n][:, cols],
                     lhsT=y_codes[n][:, t * P : (t + 1) * P].bitcast(FP8X4),
                     lhsT_scale=y_scales[n][:, t * P : (t + 1) * P],
-                    rhs=s_codes[n][:, t * B * SLOTS : (t + 1) * B * SLOTS].bitcast(FP8X4),
-                    rhs_scale=s_scales[n][:, t * B * SLOTS : (t + 1) * B * SLOTS],
+                    rhs=s_codes[n][:, cols].bitcast(FP8X4),
+                    rhs_scale=s_scales[n][:, cols],
                     start=True,
                     stop=True,
                 )
-            return crossed
 
-        def pick(n, crossed):
+        def pick(n):
             if not 0 <= n < STEPS:
                 return
             own = two.tile([P, T, QUAD_GROUPS, SLOTS], F32)
+            by_group = crossed[n][:].rearrange("q (t b x) -> q t b x", t=T, b=B)
             for a in range(P // QUAD):
                 rows = slice(a * QUAD, (a + 1) * QUAD)
                 groups = slice(a * QUAD_GROUPS, (a + 1) * QUAD_GROUPS)
                 nc.vector.tensor_tensor(
                     out=own[rows],
-                    in0=crossed[rows, :, groups, :],
+                    in0=by_group[rows, :, groups, :],
                     in1=own_group[rows].unsqueeze(1).unsqueeze(3).to_broadcast([QUAD, T, QUAD_GROUPS, SLOTS]),
                     op=ALU.mult,
                 )
@@ -311,9 +318,12 @@ def tile_hierarchicalsoftmoe2dblock_pb_t_kernel(tc, yn, means, w_slot2, out_0, o
             k_next, quarter = divmod(w_at, 4)
 
             turn_tokens(n + 1, 2 * m)
-            turn_slots(unit - 2)
-            multiply_means(unit)
+            multiply_means(unit, 0)
+            cross(n - 2, 2 * m)
             sum_squares(unit, 0)
+            turn_slots(unit - 2)
+            multiply_means(unit, 1)
+            cross(n - 2, 2 * m + 1)
             sum_squares(unit, 1)
             invert_norms(unit)
             if quarter == 2:
@@ -326,12 +336,11 @@ def tile_hierarchicalsoftmoe2dblock_pb_t_kernel(tc, yn, means, w_slot2, out_0, o
             normalise(unit - 1, 1, m == 0)
             turn_tokens(n + 1, 2 * m + 1)
             if m == 1:
-                crossed = cross(n - 2)
                 turn_means(n + 2)
-                pick(n - 2, crossed)
+                pick(n - 2)
+                quantise_slots(n - 1)
             else:
                 quantise_means(n + 1)
-                quantise_slots(n - 2)
 
             if m == 1 and n >= -2:
                 load_means(n + 6)

@@ -29,6 +29,8 @@ B = 16
 QUAD = 32
 QUAD_GROUPS = QUAD // TOKENS
 CROSS_COLUMNS = 256
+PARTS = ((0, 8),)
+AHEAD = 2
 EPS = 1e-6
 
 FLOPS = 2 * STEPS * P * SEGMENTS * D * INNER * D + 2 * STEPS * P * TOKENS * SLOTS * D
@@ -59,18 +61,20 @@ def tile_hierarchicalsoftmoe2dblock_pb_t_kernel(tc, yn, means, w_slot2, out_0, o
         y_grouped, y_codes, y_scales = {}, {}, {}
         s_grouped, s_codes, s_scales = {}, {}, {}
         se_banks, square_sums, inv_norms, se2_rows, crossed = {}, {}, {}, {}, {}
+        m_turned, y_turned, s_turned = {}, {}, {}
+        spread, tops, shifteds, totals = {}, {}, {}, {}
 
-        def load_w(k, pieces):
+        def load_w(k, part=0, parts=1):
             if not 0 <= k < EXPERTS:
                 return
-            w_in = w_pool.tile([P, PACK, INNER * D], BF16)
-            width = INNER * D // pieces
-            for i in range(pieces):
-                cols = slice(i * width, (i + 1) * width)
-                nc.sync.dma_start(
-                    out=w_in[:, :, cols], in_=w_slot2[k].rearrange("(p j) c -> p j c", j=PACK)[:, :, cols]
-                )
-            w_raw[k] = w_in
+            if part == 0:
+                w_in = w_pool.tile([P, PACK, INNER * D], BF16)
+                w_raw[k] = w_in
+            width = INNER * D // parts
+            cols = slice(part * width, (part + 1) * width)
+            nc.sync.dma_start(
+                out=w_raw[k][:, :, cols], in_=w_slot2[k].rearrange("(p j) c -> p j c", j=PACK)[:, :, cols]
+            )
 
         def load_means(n):
             if not 0 <= n < STEPS:
@@ -80,13 +84,15 @@ def tile_hierarchicalsoftmoe2dblock_pb_t_kernel(tc, yn, means, w_slot2, out_0, o
             nc.sync.dma_start(out=m_in[:], in_=means_rows[k, h * P : (h + 1) * P, :])
             m_raw[n] = m_in
 
-        def load_tokens(n):
+        def load_tokens(n, part=0, parts=1):
             if not 0 <= n < STEPS:
                 return
             k, h = divmod(n, HALVES)
-            y_in = y_pool.tile([P, TOKENS * D], BF16)
-            nc.sync.dma_start(out=y_in[:], in_=yn_rows[k, h * P : (h + 1) * P, :])
-            y_raw[n] = y_in
+            if part == 0:
+                y_in = y_pool.tile([P, TOKENS * D], BF16)
+                y_raw[n] = y_in
+            cols = slice(part * TOKENS * D // parts, (part + 1) * TOKENS * D // parts)
+            nc.sync.dma_start(out=y_raw[n][:, cols], in_=yn_rows[k, h * P : (h + 1) * P, cols])
 
         def regroup_w(k, i, on_scalar):
             if not 0 <= k < EXPERTS:
@@ -112,8 +118,6 @@ def tile_hierarchicalsoftmoe2dblock_pb_t_kernel(tc, yn, means, w_slot2, out_0, o
             w_codes[k, e], w_scales[k, e] = codes, scales
 
         def turn_means(n):
-            if not 0 <= n < STEPS:
-                return
             words = m_raw[n][:].bitcast(F32)
             turned = turned_ps.tile([P, SEGMENTS, 2, P], F32)
             for m in range(SEGMENTS):
@@ -121,10 +125,13 @@ def tile_hierarchicalsoftmoe2dblock_pb_t_kernel(tc, yn, means, w_slot2, out_0, o
                     nc.tensor.transpose(
                         turned[:, m, u, :], words[:, m * WORDS + u : (m + 1) * WORDS : 2], ident[:]
                     )
+            m_turned[n] = turned
+
+        def copy_means(n):
             m_new = two.tile([P, SEGMENTS * P * PACK], BF16, align_bytes=64, name="m_grouped")
             nc.scalar.copy(
                 out=m_new[:].bitcast(F32).rearrange("p (m c u) -> p m c u", c=P, u=2),
-                in_=turned[:].rearrange("p m u c -> p m c u"),
+                in_=m_turned[n][:].rearrange("p m u c -> p m c u"),
             )
             m_grouped[n] = m_new
 
@@ -137,19 +144,22 @@ def tile_hierarchicalsoftmoe2dblock_pb_t_kernel(tc, yn, means, w_slot2, out_0, o
             m_codes[n], m_scales[n] = codes, scales
 
         def turn_tokens(n, i):
-            if not 0 <= n < STEPS:
-                return
-            if i == 0:
-                y_new = two.tile([P, P * TOKENS * PACK], BF16, align_bytes=64, name="y_grouped")
-                y_grouped[n] = y_new
             words = y_raw[n][:].bitcast(F32)
             turned = turned_ps.tile([P, 2, 2, P], F32)
             for s in range(2):
                 for u in range(2):
                     row = 2 * i + s
                     nc.tensor.transpose(turned[:, s, u, :], words[:, row * WORDS + u : (row + 1) * WORDS : 2], ident[:])
+            y_turned[n, i] = turned
+
+        def copy_tokens(n, i):
+            if i == 0:
+                y_new = two.tile([P, P * TOKENS * PACK], BF16, align_bytes=64, name="y_grouped")
+                y_grouped[n] = y_new
             pairs = y_grouped[n][:].bitcast(F32).rearrange("p (g s u) -> p g s u", s=TOKENS, u=2)
-            nc.scalar.copy(out=pairs[:, :, 2 * i : 2 * i + 2, :], in_=turned[:].rearrange("p s u g -> p g s u"))
+            nc.scalar.copy(
+                out=pairs[:, :, 2 * i : 2 * i + 2, :], in_=y_turned[n, i][:].rearrange("p s u g -> p g s u")
+            )
 
         def quantise_tokens(n, part):
             if not 0 <= n < STEPS:
@@ -222,20 +232,21 @@ def tile_hierarchicalsoftmoe2dblock_pb_t_kernel(tc, yn, means, w_slot2, out_0, o
                 )
 
         def turn_slots(unit):
-            if not 0 <= unit < UNITS:
-                return
-            n, m = divmod(unit, SEGMENTS)
-            if m == 0:
-                s_new = two.tile([P, P * SLOTS * PACK], BF16, align_bytes=64, name="s_grouped")
-                s_grouped[n] = s_new
             words = se2_rows[unit][:].bitcast(F32)
             turned = turned_ps.tile([P, INNER, 2, P], F32)
             for e in range(INNER):
                 for u in range(2):
                     first = e * WORDS + u * P
                     nc.tensor.transpose(turned[:, e, u, :], words[:, first : first + P], ident[:])
+            s_turned[unit] = turned
+
+        def copy_slots(unit):
+            n, m = divmod(unit, SEGMENTS)
+            if m == 0:
+                s_new = two.tile([P, P * SLOTS * PACK], BF16, align_bytes=64, name="s_grouped")
+                s_grouped[n] = s_new
             pairs = s_grouped[n][:].bitcast(F32).rearrange("p (g m e u) -> p m g e u", m=SEGMENTS, e=INNER, u=2)
-            nc.scalar.copy(out=pairs[:, m], in_=turned[:].rearrange("p e u g -> p g e u"))
+            nc.scalar.copy(out=pairs[:, m], in_=s_turned[unit][:].rearrange("p e u g -> p g e u"))
 
         def quantise_slots(n):
             if not 0 <= n < STEPS:
@@ -270,132 +281,206 @@ def tile_hierarchicalsoftmoe2dblock_pb_t_kernel(tc, yn, means, w_slot2, out_0, o
         def pick(n):
             if not 0 <= n < STEPS:
                 return
-            own = two.tile([P, T, QUAD_GROUPS, SLOTS], F32)
-            by_group = crossed[n][:].rearrange("q (t b x) -> q t b x", t=T, b=B)
+            k, h = divmod(n, HALVES)
+            part = [k0 <= k < k1 for k0, k1 in PARTS].index(True)
+            first = ((k - PARTS[part][0]) * HALVES + h) * T
+            by_group = crossed[n][:].rearrange("q (t b x) -> q x b t", t=T, b=B)
             for a in range(P // QUAD):
                 rows = slice(a * QUAD, (a + 1) * QUAD)
                 groups = slice(a * QUAD_GROUPS, (a + 1) * QUAD_GROUPS)
+                nc.scalar.copy(out=candidates[part][rows, :, :, first : first + T], in_=by_group[rows, :, groups, :])
+
+        def spread_part(part, j):
+            k0, k1 = PARTS[part]
+            width = (k1 - k0) * HALVES * T
+            span = P // width
+            if j >= QUAD_GROUPS // span:
+                return
+            if j == 0:
+                x = last.tile([P, SLOTS, B // span, TOKENS], F32, name="spread")
+                spread[part] = x
+            turned = turned_ps.tile([P, SLOTS, P], F32)
+            flat = candidates[part][:].rearrange("q x c r -> q x (c r)")
+            for slot in range(SLOTS):
+                e, m = divmod(slot, SEGMENTS)
+                nc.tensor.transpose(turned[:, slot, :], flat[:, INNER * m + e, j * P : (j + 1) * P], ident[:])
+            by_c = turned[:].rearrange("r slot (a c s) -> r slot c a s", c=QUAD_GROUPS, s=TOKENS)
+            chosen = spread[part][:].rearrange("r slot (a j) s -> r slot j a s", j=QUAD_GROUPS // span)
+            for c in range(span):
+                rows = slice(c * width, (c + 1) * width)
+                nc.vector.tensor_copy(out=chosen[rows, :, j], in_=by_c[rows, :, span * j + c])
+
+        def softmax_views(part):
+            groups = spread[part].shape[2]
+            full = [P, SLOTS, groups, TOKENS]
+            over_tokens = (out_0, lambda x: x, [P, SLOTS, groups], lambda x: x.unsqueeze(3).to_broadcast(full))
+            over_slots = (
+                out_1,
+                lambda x: x.rearrange("r slot g s -> r g s slot"),
+                [P, groups, TOKENS],
+                lambda x: x.unsqueeze(1).to_broadcast(full),
+            )
+            return over_tokens, over_slots
+
+        def find_tops(part):
+            for i, (out, index_last, reduced_shape, repeated) in enumerate(softmax_views(part)):
+                top = last.tile(reduced_shape, F32, name="top%d" % i)
+                nc.vector.tensor_reduce(out=top[:], in_=index_last(spread[part][:]), axis=AXIS.X, op=ALU.max)
+                tops[part, i] = top
+
+        def exponentiate(part):
+            for i, (out, index_last, reduced_shape, repeated) in enumerate(softmax_views(part)):
+                shifted = last.tile(spread[part].shape, F32, name="shifted%d" % i)
                 nc.vector.tensor_tensor(
-                    out=own[rows],
-                    in0=by_group[rows, :, groups, :],
-                    in1=own_group[rows].unsqueeze(1).unsqueeze(3).to_broadcast([QUAD, T, QUAD_GROUPS, SLOTS]),
+                    out=shifted[:], in0=spread[part][:], in1=repeated(tops[part, i][:]), op=ALU.subtract
+                )
+                nc.scalar.activation(out=shifted[:], in_=shifted[:], func=ACT.Exp)
+                shifteds[part, i] = shifted
+
+        def invert_totals(part):
+            for i, (out, index_last, reduced_shape, repeated) in enumerate(softmax_views(part)):
+                total = last.tile(reduced_shape, F32, name="total%d" % i)
+                nc.vector.tensor_reduce(out=total[:], in_=index_last(shifteds[part, i][:]), axis=AXIS.X, op=ALU.add)
+                nc.vector.reciprocal(out=total[:], in_=total[:])
+                totals[part, i] = total
+
+        def finish(part, queues):
+            k0, k1 = PARTS[part]
+            rows = HALVES * T
+            span = P // ((k1 - k0) * rows)
+            for i, (out, index_last, reduced_shape, repeated) in enumerate(softmax_views(part)):
+                weights = last.tile([P, B // span, TOKENS, SLOTS], F32, name="weights%d" % i)
+                nc.vector.tensor_tensor(
+                    out=weights[:],
+                    in0=shifteds[part, i][:].rearrange("r slot g s -> r g s slot"),
+                    in1=repeated(totals[part, i][:]).rearrange("r slot g s -> r g s slot"),
                     op=ALU.mult,
                 )
-            nc.vector.tensor_reduce(
-                out=logits[:].rearrange("q (e m) r -> q r m e", m=SEGMENTS)[:, n * T : (n + 1) * T],
-                in_=own[:].rearrange("q t c (m e) -> q t m e c", e=INNER),
-                axis=AXIS.X,
-                op=ALU.add,
-            )
-
-        load_w(0, 2)
-        load_means(0)
-        load_tokens(0)
-        load_means(1)
-        load_tokens(1)
-        load_w(1, 2)
-        load_means(2)
-        load_tokens(2)
-        load_means(3)
-        load_tokens(3)
-        load_w(2, 1)
+                per_expert = out.rearrange("x g k s slot -> k (x g) (s slot)")
+                for c in range(span):
+                    for k in range(k0, k1):
+                        first = (c * (k1 - k0) + k - k0) * rows
+                        queues[i].dma_start(
+                            out=per_expert[k].rearrange("(r g c) w -> c r g w", c=span, r=rows)[c],
+                            in_=weights[first : first + rows].rearrange("r g s slot -> r g (s slot)"),
+                        )
 
         ident = consts.tile([P, P], F32)
         make_identity(nc, ident[:])
-        own_group = consts.tile([P, QUAD_GROUPS], F32)
-        nc.vector.tensor_reduce(
-            out=own_group[:],
-            in_=ident[:].rearrange("q (a c s) -> q c a s", c=QUAD_GROUPS, s=TOKENS),
-            axis=AXIS.XY,
-            op=ALU.add,
-        )
-        logits = consts.tile([P, SLOTS, STEPS * T], F32)
+        candidates = []
+        for part, (k0, k1) in enumerate(PARTS):
+            held = consts.tile([P, SLOTS, QUAD_GROUPS, (k1 - k0) * HALVES * T], F32, name="candidates%d" % part)
+            candidates.append(held)
 
-        for unit in range(-5, UNITS + 4):
+        uses = [(turn_means, copy_means, (0,))]
+        for i in range(4):
+            uses.append((turn_tokens, copy_tokens, (0, i)))
+        uses.append((turn_means, copy_means, (1,)))
+        uses.append((turn_tokens, copy_tokens, (1, 0)))
+        for unit in range(UNITS + 2):
             n, m = divmod(unit, SEGMENTS)
-            filling = unit < 0
-            w_at = unit + 5
-            k_next, quarter = divmod(w_at, 4)
+            if n + 1 < STEPS and unit > 0:
+                uses.append((turn_tokens, copy_tokens, (n + 1, 2 * m)))
+            if unit >= 2:
+                uses.append((turn_slots, copy_slots, (unit - 2,)))
+            if n + 1 < STEPS:
+                uses.append((turn_tokens, copy_tokens, (n + 1, 2 * m + 1)))
+            if m == 0 and n + 2 < STEPS:
+                uses.append((turn_means, copy_means, (n + 2,)))
+        done = [0, 0]
 
-            turn_tokens(n + 1, 2 * m)
-            multiply_means(unit, 0)
-            cross(n - 2, 2 * m)
-            sum_squares(unit, 0)
-            turn_slots(unit - 2)
-            multiply_means(unit, 1)
-            cross(n - 2, 2 * m + 1)
+        def copy_out():
+            while done[0] < min(done[1] + AHEAD + 1, len(uses)):
+                turn, copy, args = uses[done[0]]
+                if turn == turn_slots and args[0] not in se2_rows:
+                    break
+                turn(*args)
+                done[0] += 1
+            turn, copy, args = uses[done[1]]
+            copy(*args)
+            done[1] += 1
+
+        load_w(0, 0, 2)
+        load_means(0)
+        load_tokens(0, 0, 2)
+        load_w(0, 1, 2)
+        load_tokens(0, 1, 2)
+        load_means(1)
+        load_tokens(1)
+        load_w(1)
+        load_means(2)
+        load_tokens(2)
+        load_means(3)
+        load_w(2)
+        load_tokens(3)
+        regroup_w(0, 0, False)
+        regroup_w(0, 1, True)
+        copy_out()
+        quantise_w(0, 0)
+        quantise_means(0)
+        copy_out()
+        multiply_means(0, 0)
+        copy_out()
+        sum_squares(0, 0)
+        regroup_w(0, 2, False)
+        regroup_w(0, 3, False)
+        copy_out()
+        quantise_w(0, 1)
+        multiply_means(0, 1)
+        copy_out()
+        copy_out()
+        quantise_means(1)
+        copy_out()
+
+        for unit in range(UNITS + 5):
+            n, m = divmod(unit, SEGMENTS)
+            quarter = (unit + 1) % 4
+            k_next = (unit + 1) // 4 + 1
+            last_w = unit // 4 + 1
+            if unit > 0:
+                sum_squares(unit, 0)
             sum_squares(unit, 1)
-            invert_norms(unit)
-            if quarter == 2:
-                quantise_w(k_next, 0)
-            if quarter == 0:
-                quantise_w(k_next - 1, 1)
-            regroup_w(k_next, quarter, filling and quarter % 2 == 1)
-            quantise_tokens(n, m)
-            normalise(unit - 1, 0, False)
-            normalise(unit - 1, 1, m == 0)
-            turn_tokens(n + 1, 2 * m + 1)
+            if m == 0:
+                quantise_slots(n - 2)
+            if n + 1 < STEPS and unit > 0:
+                copy_out()
             if m == 1:
-                turn_means(n + 2)
+                for part in range(4):
+                    cross(n - 2, part)
+            invert_norms(unit)
+            if 2 <= unit < UNITS + 2:
+                copy_out()
+            normalise(unit - 1, 0, False)
+            normalise(unit - 1, 1, False)
+            if m == 1:
+                quantise_means(n + 2)
+            if unit % 4 == 1:
+                quantise_w(last_w, 0)
+            if unit % 4 == 3:
+                quantise_w(last_w, 1)
+            quantise_tokens(n, m)
+            multiply_means(unit + 1, 0)
+            multiply_means(unit + 1, 1)
+            if n + 1 < STEPS:
+                copy_out()
+            if unit == 0:
+                regroup_w(1, 0, False)
+            regroup_w(k_next, quarter, False)
+            if m == 0 and n + 2 < STEPS:
+                copy_out()
+            if m == 1:
                 pick(n - 2)
-                quantise_slots(n - 1)
+            if m == 0:
+                load_tokens(n + 4)
             else:
-                quantise_means(n + 1)
+                load_means(n + 4)
+                if unit % 4 == 3:
+                    load_w(last_w + 2)
 
-            if m == 1 and n >= -2:
-                load_means(n + 6)
-            if m == 1 and n >= -1:
-                load_tokens(n + 5)
-            if quarter == 3:
-                load_w(k_next + 3, 1)
-
-        by_row_ps = logit_ps.tile([P, SLOTS, P], F32, tag="crossed")
-        for slot in range(SLOTS):
-            nc.tensor.transpose(by_row_ps[:, slot, :], logits[:, slot, :], ident[:])
-        by_row = by_row_ps[:].rearrange("r slot (b s) -> r slot b s", b=B)
-        full = [P, SLOTS, B, TOKENS]
-        over_tokens = (
-            out_0,
-            nc.sync,
-            lambda x: x,
-            [P, SLOTS, B],
-            lambda x: x.unsqueeze(3).to_broadcast(full),
-        )
-        over_slots = (
-            out_1,
-            nc.scalar,
-            lambda x: x.rearrange("r slot b s -> r b s slot"),
-            [P, B, TOKENS],
-            lambda x: x.unsqueeze(1).to_broadcast(full),
-        )
-        both = (over_tokens, over_slots)
-        tops, shifteds, totals = [], [], []
-        for out, queue, index_last, reduced_shape, repeated in both:
-            top = last.tile(reduced_shape, F32)
-            nc.vector.tensor_reduce(out=top[:], in_=index_last(by_row), axis=AXIS.X, op=ALU.max)
-            tops.append(top)
-        for (out, queue, index_last, reduced_shape, repeated), top in zip(both, tops):
-            shifted = last.tile(full, F32)
-            nc.vector.tensor_tensor(out=shifted[:], in0=by_row, in1=repeated(top[:]), op=ALU.subtract)
-            nc.scalar.activation(out=shifted[:], in_=shifted[:], func=ACT.Exp)
-            shifteds.append(shifted)
-        for (out, queue, index_last, reduced_shape, repeated), shifted in zip(both, shifteds):
-            total = last.tile(reduced_shape, F32)
-            nc.vector.tensor_reduce(out=total[:], in_=index_last(shifted[:]), axis=AXIS.X, op=ALU.add)
-            nc.vector.reciprocal(out=total[:], in_=total[:])
-            totals.append(total)
-        for (out, queue, index_last, reduced_shape, repeated), shifted, total in zip(both, shifteds, totals):
-            weights = last.tile([P, B, TOKENS, SLOTS], F32)
-            nc.vector.tensor_tensor(
-                out=weights[:],
-                in0=shifted[:].rearrange("r slot b s -> r b s slot"),
-                in1=repeated(total[:]).rearrange("r slot b s -> r b s slot"),
-                op=ALU.mult,
-            )
-            per_expert = out.rearrange("x g k s slot -> k (x g) (s slot)")
-            rows = HALVES * T
-            for k in range(EXPERTS):
-                queue.dma_start(
-                    out=per_expert[k].rearrange("(r b) w -> r b w", b=B),
-                    in_=weights[k * rows : (k + 1) * rows].rearrange("r b s slot -> r b (s slot)"),
-                )
+        end = len(PARTS) - 1
+        for j in range(QUAD_GROUPS):
+            spread_part(end, j)
+        find_tops(end)
+        exponentiate(end)
+        invert_totals(end)
+        finish(end, (nc.sync, nc.scalar))

@@ -28,9 +28,10 @@ T = 8
 B = 16
 QUAD = 32
 QUAD_GROUPS = QUAD // TOKENS
-CROSS_COLUMNS = 256
+CROSS_COLUMNS = 128
 PARTS = ((0, 8),)
 AHEAD = 2
+DUPS = ((2, 2), (2, 2))
 EPS = 1e-6
 
 FLOPS = 2 * STEPS * P * SEGMENTS * D * INNER * D + 2 * STEPS * P * TOKENS * SLOTS * D
@@ -157,7 +158,8 @@ def tile_hierarchicalsoftmoe2dblock_pb_t_kernel(tc, yn, means, w_slot2, out_0, o
                 y_new = two.tile([P, P * TOKENS * PACK], BF16, align_bytes=64, name="y_grouped")
                 y_grouped[n] = y_new
             pairs = y_grouped[n][:].bitcast(F32).rearrange("p (g s u) -> p g s u", s=TOKENS, u=2)
-            nc.scalar.copy(
+            engine = nc.vector.tensor_copy if i == 2 else nc.scalar.copy
+            engine(
                 out=pairs[:, :, 2 * i : 2 * i + 2, :], in_=y_turned[n, i][:].rearrange("p s u g -> p g s u")
             )
 
@@ -181,15 +183,16 @@ def tile_hierarchicalsoftmoe2dblock_pb_t_kernel(tc, yn, means, w_slot2, out_0, o
             n, m = divmod(unit, SEGMENTS)
             k = n // HALVES
             se = rows_ps.tile([P, D], F32)
-            nc.tensor.matmul_mx(
-                out=se[:],
-                lhsT=m_codes[n][:, m * P : (m + 1) * P].bitcast(FP8X4),
-                lhsT_scale=m_scales[n][:, m * P : (m + 1) * P],
-                rhs=w_codes[k, e][:].bitcast(FP8X4),
-                rhs_scale=w_scales[k, e][:],
-                start=True,
-                stop=True,
-            )
+            for again in range(2):
+                nc.tensor.matmul_mx(
+                    out=se[:],
+                    lhsT=m_codes[n][:, m * P : (m + 1) * P].bitcast(FP8X4),
+                    lhsT_scale=m_scales[n][:, m * P : (m + 1) * P],
+                    rhs=w_codes[k, e][:].bitcast(FP8X4),
+                    rhs_scale=w_scales[k, e][:],
+                    start=True,
+                    stop=True,
+                )
             se_banks[unit, e] = se
 
         def sum_squares(unit, e):
@@ -256,13 +259,13 @@ def tile_hierarchicalsoftmoe2dblock_pb_t_kernel(tc, yn, means, w_slot2, out_0, o
             nc.vector.quantize_mx(out=codes[:].bitcast(FP8X4), scales=scales[:], in_=s_grouped[n][:])
             s_codes[n], s_scales[n] = codes, scales
 
-        def cross(n, part):
+        def cross(n, t0, t1):
             if not 0 <= n < STEPS:
                 return
-            if part == 0:
+            if t0 == 0:
                 crossed_new = logit_ps.tile([P, T * B * SLOTS], F32, name="crossed")
                 crossed[n] = crossed_new
-            for t in range(2 * part, 2 * part + 2):
+            for t in range(t0, t1):
                 first = t * B * SLOTS
                 width = B * SLOTS
                 while width < CROSS_COLUMNS and first + 2 * width <= T * B * SLOTS:
@@ -372,25 +375,28 @@ def tile_hierarchicalsoftmoe2dblock_pb_t_kernel(tc, yn, means, w_slot2, out_0, o
             held = consts.tile([P, SLOTS, QUAD_GROUPS, (k1 - k0) * HALVES * T], F32, name="candidates%d" % part)
             candidates.append(held)
 
-        uses = [(turn_means, copy_means, (0,))]
-        for i in range(4):
-            uses.append((turn_tokens, copy_tokens, (0, i)))
-        uses.append((turn_means, copy_means, (1,)))
-        uses.append((turn_tokens, copy_tokens, (1, 0)))
-        for unit in range(UNITS + 2):
+        uses = [(turn_means, copy_means, (0,)), (turn_means, copy_means, (1,))]
+
+        def on(unit):
+            return 0 <= unit < UNITS
+
+        def listed(turn, copy, *args):
+            uses.append((turn, copy, args))
+
+        for unit in range(UNITS + 8):
             n, m = divmod(unit, SEGMENTS)
-            if n + 1 < STEPS and unit > 0:
-                uses.append((turn_tokens, copy_tokens, (n + 1, 2 * m)))
-            if unit >= 2:
-                uses.append((turn_slots, copy_slots, (unit - 2,)))
-            if n + 1 < STEPS:
-                uses.append((turn_tokens, copy_tokens, (n + 1, 2 * m + 1)))
-            if m == 0 and n + 2 < STEPS:
-                uses.append((turn_means, copy_means, (n + 2,)))
+            if on(unit - 1):
+                listed(turn_tokens, copy_tokens, (unit - 1) // 2, 2 * ((unit - 1) % 2))
+            if on(unit - 2):
+                listed(turn_slots, copy_slots, unit - 2)
+            if on(unit - 1):
+                listed(turn_tokens, copy_tokens, (unit - 1) // 2, 2 * ((unit - 1) % 2) + 1)
+            if (unit + 4) % 2 == 0 and on(unit + 4) and unit >= 0:
+                listed(turn_means, copy_means, (unit + 4) // 2)
         done = [0, 0]
 
-        def copy_out():
-            while done[0] < min(done[1] + AHEAD + 1, len(uses)):
+        def copy_out(ahead=AHEAD):
+            while done[0] < min(done[1] + ahead + 1, len(uses)):
                 turn, copy, args = uses[done[0]]
                 if turn == turn_slots and args[0] not in se2_rows:
                     break
@@ -400,82 +406,75 @@ def tile_hierarchicalsoftmoe2dblock_pb_t_kernel(tc, yn, means, w_slot2, out_0, o
             copy(*args)
             done[1] += 1
 
-        load_w(0, 0, 2)
+        load_w(0, 0, 4)
+        load_w(0, 1, 4)
         load_means(0)
-        load_tokens(0, 0, 2)
         load_w(0, 1, 2)
-        load_tokens(0, 1, 2)
         load_means(1)
-        load_tokens(1)
-        load_w(1)
+        load_tokens(0, 0, 2)
+        load_w(1, 0, 2)
         load_means(2)
-        load_tokens(2)
+        load_tokens(0, 1, 2)
+        load_w(1, 1, 2)
+        load_tokens(1)
         load_means(3)
         load_w(2)
-        load_tokens(3)
         regroup_w(0, 0, False)
         regroup_w(0, 1, True)
-        copy_out()
+        copy_out(1)
         quantise_w(0, 0)
         quantise_means(0)
-        copy_out()
         multiply_means(0, 0)
-        copy_out()
-        sum_squares(0, 0)
         regroup_w(0, 2, False)
-        regroup_w(0, 3, False)
-        copy_out()
+        regroup_w(0, 3, True)
         quantise_w(0, 1)
         multiply_means(0, 1)
-        copy_out()
-        copy_out()
+        copy_out(1)
         quantise_means(1)
-        copy_out()
+        regroup_w(1, 0, False)
 
-        for unit in range(UNITS + 5):
-            n, m = divmod(unit, SEGMENTS)
-            quarter = (unit + 1) % 4
-            k_next = (unit + 1) // 4 + 1
-            last_w = unit // 4 + 1
+        for unit in range(UNITS + 8):
+            sum_squares(unit, 0)
+            if (unit - 4) % 2 == 0:
+                quantise_slots((unit - 4) // 2)
             if unit > 0:
-                sum_squares(unit, 0)
-            sum_squares(unit, 1)
-            if m == 0:
-                quantise_slots(n - 2)
-            if n + 1 < STEPS and unit > 0:
+                multiply_means(unit, 1)
+            if (unit - 5) % 2 == 0:
+                cross((unit - 5) // 2, 3, 6)
+            if on(unit - 1):
                 copy_out()
-            if m == 1:
-                for part in range(4):
-                    cross(n - 2, part)
-            invert_norms(unit)
-            if 2 <= unit < UNITS + 2:
+            if on(unit - 2):
                 copy_out()
             normalise(unit - 1, 0, False)
             normalise(unit - 1, 1, False)
-            if m == 1:
-                quantise_means(n + 2)
-            if unit % 4 == 1:
-                quantise_w(last_w, 0)
-            if unit % 4 == 3:
-                quantise_w(last_w, 1)
-            quantise_tokens(n, m)
+            if (unit - 6) % 2 == 0:
+                pick((unit - 6) // 2)
+            sum_squares(unit, 1)
             multiply_means(unit + 1, 0)
-            multiply_means(unit + 1, 1)
-            if n + 1 < STEPS:
+            if (unit - 4) % 2 == 0:
+                cross((unit - 4) // 2, 0, 3)
+            if (unit - 5) % 2 == 0:
+                cross((unit - 5) // 2, 6, 8)
+            if (unit + 3) % 2 == 0 and unit > 0:
+                quantise_means((unit + 3) // 2)
+            if unit % 4 == 1:
+                quantise_w(unit // 4 + 1, 0)
+            if unit % 4 == 3:
+                quantise_w(unit // 4 + 1, 1)
+            if on(unit - 3):
+                quantise_tokens((unit - 3) // 2, (unit - 3) % 2)
+            if on(unit - 1):
                 copy_out()
-            if unit == 0:
-                regroup_w(1, 0, False)
-            regroup_w(k_next, quarter, False)
-            if m == 0 and n + 2 < STEPS:
+            invert_norms(unit)
+            regroup_w((unit + 1) // 4 + 1, (unit + 1) % 4, False)
+            if (unit + 4) % 2 == 0 and on(unit + 4) and unit >= 0:
                 copy_out()
-            if m == 1:
-                pick(n - 2)
-            if m == 0:
-                load_tokens(n + 4)
+            if unit % 2 == 0:
+                load_tokens((unit - 1) // 2 + 3)
             else:
-                load_means(n + 4)
+                load_means(unit // 2 + 4)
                 if unit % 4 == 3:
-                    load_w(last_w + 2)
+                    load_w(unit // 4 + 3)
 
         end = len(PARTS) - 1
         for j in range(QUAD_GROUPS):

@@ -31,7 +31,7 @@ QUAD_GROUPS = QUAD // TOKENS
 CROSS_COLUMNS = 128
 PARTS = ((0, 8),)
 AHEAD = 2
-DUPS = ((2, 2), (2, 2))
+FIRST_PASSES = 2
 EPS = 1e-6
 
 FLOPS = 2 * STEPS * P * SEGMENTS * D * INNER * D + 2 * STEPS * P * TOKENS * SLOTS * D
@@ -47,6 +47,7 @@ def tile_hierarchicalsoftmoe2dblock_pb_t_kernel(tc, yn, means, w_slot2, out_0, o
         w_pool = ctx.enter_context(tc.tile_pool(name="w_pool", bufs=3))
         m_pool = ctx.enter_context(tc.tile_pool(name="m_pool", bufs=4))
         y_pool = ctx.enter_context(tc.tile_pool(name="y_pool", bufs=4))
+        w_ring = ctx.enter_context(tc.tile_pool(name="w_ring", bufs=3))
         two = ctx.enter_context(tc.tile_pool(name="two", bufs=2))
         three = ctx.enter_context(tc.tile_pool(name="three", bufs=3))
         small = ctx.enter_context(tc.tile_pool(name="small", bufs=4))
@@ -95,28 +96,40 @@ def tile_hierarchicalsoftmoe2dblock_pb_t_kernel(tc, yn, means, w_slot2, out_0, o
             cols = slice(part * TOKENS * D // parts, (part + 1) * TOKENS * D // parts)
             nc.sync.dma_start(out=y_raw[n][:, cols], in_=yn_rows[k, h * P : (h + 1) * P, cols])
 
-        def regroup_w(k, i, on_scalar):
+        def regroup_w(k, i, engine):
+            if not 0 <= k < EXPERTS:
+                return
+            e, part = divmod(i, 2)
+            width = D // 2
+            w_new = w_ring.tile([P, width * PACK], BF16, align_bytes=64, name="w_grouped")
+            w_grouped[k, i] = w_new
+            dst = w_new[:]
+            src = w_raw[k][:, :, i * width : (i + 1) * width]
+            if engine == nc.gpsimd:
+                nc.gpsimd.tensor_scalar(
+                    out=dst.rearrange("p (c j) -> p c j", j=PACK),
+                    in0=src.rearrange("p j c -> p c j"),
+                    scalar1=1.0,
+                    scalar2=0.0,
+                    op0=ALU.mult,
+                    op1=ALU.add,
+                )
+                return
+            copy = nc.scalar.copy if engine == nc.scalar else nc.vector.tensor_copy
+            copy(out=dst.rearrange("p (c j) -> p c j", j=PACK), in_=src.rearrange("p j c -> p c j"))
+
+        def quantise_quarter(k, i):
             if not 0 <= k < EXPERTS:
                 return
             e, part = divmod(i, 2)
             if part == 0:
-                w_new = three.tile([P, D * PACK], BF16, align_bytes=64, name="w_grouped")
-                w_grouped[k, e] = w_new
-            width = D // 2
-            dst = w_grouped[k, e][:].rearrange("p (c j) -> p c j", j=PACK)[:, part * width : (part + 1) * width, :]
-            src = w_raw[k][:].rearrange("p j c -> p c j")[:, i * width : (i + 1) * width, :]
-            if on_scalar:
-                nc.scalar.copy(out=dst, in_=src)
-            else:
-                nc.vector.tensor_copy(out=dst, in_=src)
-
-        def quantise_w(k, e):
-            if not 0 <= k < EXPERTS:
-                return
-            codes = two.tile([P, D], U32, align_bytes=64, name="w_codes%d" % e)
-            scales = two.tile([P, D], U8, align_bytes=64, name="w_scales%d" % e)
-            nc.vector.quantize_mx(out=codes[:].bitcast(FP8X4), scales=scales[:], in_=w_grouped[k, e][:])
-            w_codes[k, e], w_scales[k, e] = codes, scales
+                codes = two.tile([P, D], U32, align_bytes=64, name="w_codes%d" % e)
+                scales = two.tile([P, D], U8, align_bytes=64, name="w_scales%d" % e)
+                w_codes[k, e], w_scales[k, e] = codes, scales
+            cols = slice(part * D // 2, (part + 1) * D // 2)
+            nc.vector.quantize_mx(
+                out=w_codes[k, e][:, cols].bitcast(FP8X4), scales=w_scales[k, e][:, cols], in_=w_grouped[k, i][:]
+            )
 
         def turn_means(n):
             words = m_raw[n][:].bitcast(F32)
@@ -158,7 +171,7 @@ def tile_hierarchicalsoftmoe2dblock_pb_t_kernel(tc, yn, means, w_slot2, out_0, o
                 y_new = two.tile([P, P * TOKENS * PACK], BF16, align_bytes=64, name="y_grouped")
                 y_grouped[n] = y_new
             pairs = y_grouped[n][:].bitcast(F32).rearrange("p (g s u) -> p g s u", s=TOKENS, u=2)
-            engine = nc.vector.tensor_copy if i == 2 else nc.scalar.copy
+            engine = nc.vector.tensor_copy if i in (2, 3) else nc.scalar.copy
             engine(
                 out=pairs[:, :, 2 * i : 2 * i + 2, :], in_=y_turned[n, i][:].rearrange("p s u g -> p g s u")
             )
@@ -183,7 +196,7 @@ def tile_hierarchicalsoftmoe2dblock_pb_t_kernel(tc, yn, means, w_slot2, out_0, o
             n, m = divmod(unit, SEGMENTS)
             k = n // HALVES
             se = rows_ps.tile([P, D], F32)
-            for again in range(2):
+            for again in range(FIRST_PASSES):
                 nc.tensor.matmul_mx(
                     out=se[:],
                     lhsT=m_codes[n][:, m * P : (m + 1) * P].bitcast(FP8X4),
@@ -368,6 +381,9 @@ def tile_hierarchicalsoftmoe2dblock_pb_t_kernel(tc, yn, means, w_slot2, out_0, o
                             in_=weights[first : first + rows].rearrange("r g s slot -> r g (s slot)"),
                         )
 
+        one = consts.tile([P, 1], F32)
+        nc.vector.memset(one[:], 1.0)
+        nc.scalar.activation(out=one[:], in_=one[:], func=ACT.Abs_reciprocal_sqrt)
         ident = consts.tile([P, P], F32)
         make_identity(nc, ident[:])
         candidates = []
@@ -384,15 +400,14 @@ def tile_hierarchicalsoftmoe2dblock_pb_t_kernel(tc, yn, means, w_slot2, out_0, o
             uses.append((turn, copy, args))
 
         for unit in range(UNITS + 8):
-            n, m = divmod(unit, SEGMENTS)
             if on(unit - 1):
                 listed(turn_tokens, copy_tokens, (unit - 1) // 2, 2 * ((unit - 1) % 2))
             if on(unit - 2):
                 listed(turn_slots, copy_slots, unit - 2)
             if on(unit - 1):
                 listed(turn_tokens, copy_tokens, (unit - 1) // 2, 2 * ((unit - 1) % 2) + 1)
-            if (unit + 4) % 2 == 0 and on(unit + 4) and unit >= 0:
-                listed(turn_means, copy_means, (unit + 4) // 2)
+            if unit % 2 == 0 and on(unit + 4):
+                listed(turn_means, copy_means, unit // 2 + 2)
         done = [0, 0]
 
         def copy_out(ahead=AHEAD):
@@ -419,24 +434,31 @@ def tile_hierarchicalsoftmoe2dblock_pb_t_kernel(tc, yn, means, w_slot2, out_0, o
         load_tokens(1)
         load_means(3)
         load_w(2)
-        regroup_w(0, 0, False)
-        regroup_w(0, 1, True)
+        regroup_w(0, 0, nc.vector)
+        regroup_w(0, 1, nc.scalar)
         copy_out(1)
-        quantise_w(0, 0)
+        quantise_quarter(0, 0)
+        quantise_quarter(0, 1)
         quantise_means(0)
         multiply_means(0, 0)
-        regroup_w(0, 2, False)
-        regroup_w(0, 3, True)
-        quantise_w(0, 1)
+        regroup_w(0, 2, nc.vector)
+        regroup_w(0, 3, nc.scalar)
+        quantise_quarter(0, 2)
+        quantise_quarter(0, 3)
         multiply_means(0, 1)
         copy_out(1)
         quantise_means(1)
-        regroup_w(1, 0, False)
+        regroup_w(1, 0, nc.gpsimd)
+        regroup_w(1, 1, nc.gpsimd)
 
         for unit in range(UNITS + 8):
             sum_squares(unit, 0)
             if (unit - 4) % 2 == 0:
                 quantise_slots((unit - 4) // 2)
+            if on(unit - 3):
+                quantise_tokens((unit - 3) // 2, (unit - 3) % 2)
+            quantise_quarter((unit + 4) // 4, (unit + 4) % 4)
+            regroup_w((unit - -2) // 4 + 1, (unit - -2) % 4, nc.gpsimd)
             if unit > 0:
                 multiply_means(unit, 1)
             if (unit - 5) % 2 == 0:
@@ -455,19 +477,12 @@ def tile_hierarchicalsoftmoe2dblock_pb_t_kernel(tc, yn, means, w_slot2, out_0, o
                 cross((unit - 4) // 2, 0, 3)
             if (unit - 5) % 2 == 0:
                 cross((unit - 5) // 2, 6, 8)
-            if (unit + 3) % 2 == 0 and unit > 0:
-                quantise_means((unit + 3) // 2)
-            if unit % 4 == 1:
-                quantise_w(unit // 4 + 1, 0)
-            if unit % 4 == 3:
-                quantise_w(unit // 4 + 1, 1)
-            if on(unit - 3):
-                quantise_tokens((unit - 3) // 2, (unit - 3) % 2)
+            if unit % 2 == 1:
+                quantise_means(unit // 2 + 2)
             if on(unit - 1):
                 copy_out()
             invert_norms(unit)
-            regroup_w((unit + 1) // 4 + 1, (unit + 1) % 4, False)
-            if (unit + 4) % 2 == 0 and on(unit + 4) and unit >= 0:
+            if unit % 2 == 0 and on(unit + 4):
                 copy_out()
             if unit % 2 == 0:
                 load_tokens((unit - 1) // 2 + 3)

@@ -47,7 +47,7 @@ def tile_hierarchicalsoftmoe2dblock_pb_t_kernel(tc, yn, means, w_slot2, out_0, o
         w_pool = ctx.enter_context(tc.tile_pool(name="w_pool", bufs=3))
         m_pool = ctx.enter_context(tc.tile_pool(name="m_pool", bufs=4))
         y_pool = ctx.enter_context(tc.tile_pool(name="y_pool", bufs=4))
-        w_ring = ctx.enter_context(tc.tile_pool(name="w_ring", bufs=3))
+        w_ring = ctx.enter_context(tc.tile_pool(name="w_ring", bufs=2))
         two = ctx.enter_context(tc.tile_pool(name="two", bufs=2))
         three = ctx.enter_context(tc.tile_pool(name="three", bufs=3))
         small = ctx.enter_context(tc.tile_pool(name="small", bufs=4))
@@ -143,7 +143,8 @@ def tile_hierarchicalsoftmoe2dblock_pb_t_kernel(tc, yn, means, w_slot2, out_0, o
 
         def copy_means(n):
             m_new = two.tile([P, SEGMENTS * P * PACK], BF16, align_bytes=64, name="m_grouped")
-            nc.scalar.copy(
+            engine = nc.scalar.copy if n < 2 else nc.vector.tensor_copy
+            engine(
                 out=m_new[:].bitcast(F32).rearrange("p (m c u) -> p m c u", c=P, u=2),
                 in_=m_turned[n][:].rearrange("p m u c -> p m c u"),
             )
@@ -171,24 +172,16 @@ def tile_hierarchicalsoftmoe2dblock_pb_t_kernel(tc, yn, means, w_slot2, out_0, o
                 y_new = two.tile([P, P * TOKENS * PACK], BF16, align_bytes=64, name="y_grouped")
                 y_grouped[n] = y_new
             pairs = y_grouped[n][:].bitcast(F32).rearrange("p (g s u) -> p g s u", s=TOKENS, u=2)
-            engine = nc.vector.tensor_copy if i in (2, 3) else nc.scalar.copy
+            engine = nc.vector.tensor_copy if i == 2 else nc.scalar.copy
             engine(
                 out=pairs[:, :, 2 * i : 2 * i + 2, :], in_=y_turned[n, i][:].rearrange("p s u g -> p g s u")
             )
 
-        def quantise_tokens(n, part):
-            if not 0 <= n < STEPS:
-                return
-            if part == 0:
-                codes = three.tile([P, T * P], U32, align_bytes=64, name="y_codes")
-                scales = three.tile([P, T * P], U8, align_bytes=64, name="y_scales")
-                y_codes[n], y_scales[n] = codes, scales
-            width = T * P // 2
-            nc.vector.quantize_mx(
-                out=y_codes[n][:, part * width : (part + 1) * width].bitcast(FP8X4),
-                scales=y_scales[n][:, part * width : (part + 1) * width],
-                in_=y_grouped[n][:, part * width * PACK : (part + 1) * width * PACK],
-            )
+        def quantise_tokens(n):
+            codes = three.tile([P, T * P], U32, align_bytes=64, name="y_codes")
+            scales = three.tile([P, T * P], U8, align_bytes=64, name="y_scales")
+            nc.vector.quantize_mx(out=codes[:].bitcast(FP8X4), scales=scales[:], in_=y_grouped[n][:])
+            y_codes[n], y_scales[n] = codes, scales
 
         def multiply_means(unit, e):
             if not 0 <= unit < UNITS:
@@ -276,7 +269,8 @@ def tile_hierarchicalsoftmoe2dblock_pb_t_kernel(tc, yn, means, w_slot2, out_0, o
             if not 0 <= n < STEPS:
                 return
             if t0 == 0:
-                crossed_new = logit_ps.tile([P, T * B * SLOTS], F32, name="crossed")
+                pool, bank = (logit_ps, "crossed") if n < STEPS - 2 else (rows_ps, "se")
+                crossed_new = pool.tile([P, T * B * SLOTS], F32, name=bank)
                 crossed[n] = crossed_new
             for t in range(t0, t1):
                 first = t * B * SLOTS
@@ -404,10 +398,10 @@ def tile_hierarchicalsoftmoe2dblock_pb_t_kernel(tc, yn, means, w_slot2, out_0, o
                 listed(turn_tokens, copy_tokens, (unit - 1) // 2, 2 * ((unit - 1) % 2))
             if on(unit - 2):
                 listed(turn_slots, copy_slots, unit - 2)
+            if unit % 2 == 1 and on(unit + 3):
+                listed(turn_means, copy_means, unit // 2 + 2)
             if on(unit - 1):
                 listed(turn_tokens, copy_tokens, (unit - 1) // 2, 2 * ((unit - 1) % 2) + 1)
-            if unit % 2 == 0 and on(unit + 4):
-                listed(turn_means, copy_means, unit // 2 + 2)
         done = [0, 0]
 
         def copy_out(ahead=AHEAD):
@@ -448,42 +442,42 @@ def tile_hierarchicalsoftmoe2dblock_pb_t_kernel(tc, yn, means, w_slot2, out_0, o
         multiply_means(0, 1)
         copy_out(1)
         quantise_means(1)
-        regroup_w(1, 0, nc.gpsimd)
+        regroup_w(1, 0, nc.vector)
         regroup_w(1, 1, nc.gpsimd)
 
         for unit in range(UNITS + 8):
             sum_squares(unit, 0)
-            if (unit - 4) % 2 == 0:
-                quantise_slots((unit - 4) // 2)
-            if on(unit - 3):
-                quantise_tokens((unit - 3) // 2, (unit - 3) % 2)
+            if (unit - 5) % 2 == 0:
+                quantise_slots((unit - 5) // 2)
+            if on(unit - 4) and unit % 2 == 0:
+                quantise_tokens(unit // 2 - 2)
+            if unit % 2 == 0 and unit > 0:
+                quantise_means(unit // 2 + 1)
             quantise_quarter((unit + 4) // 4, (unit + 4) % 4)
-            regroup_w((unit - -2) // 4 + 1, (unit - -2) % 4, nc.gpsimd)
+            regroup_w((unit + 2) // 4 + 1, (unit + 2) % 4, nc.gpsimd)
             if unit > 0:
                 multiply_means(unit, 1)
-            if (unit - 5) % 2 == 0:
-                cross((unit - 5) // 2, 3, 6)
+            if (unit - 6) % 2 == 0:
+                cross((unit - 6) // 2, 3, 6)
             if on(unit - 1):
                 copy_out()
             if on(unit - 2):
                 copy_out()
             normalise(unit - 1, 0, False)
             normalise(unit - 1, 1, False)
-            if (unit - 6) % 2 == 0:
-                pick((unit - 6) // 2)
+            if (unit - 7) % 2 == 0:
+                pick((unit - 7) // 2)
             sum_squares(unit, 1)
             multiply_means(unit + 1, 0)
-            if (unit - 4) % 2 == 0:
-                cross((unit - 4) // 2, 0, 3)
             if (unit - 5) % 2 == 0:
-                cross((unit - 5) // 2, 6, 8)
-            if unit % 2 == 1:
-                quantise_means(unit // 2 + 2)
+                cross((unit - 5) // 2, 0, 3)
+            if (unit - 6) % 2 == 0:
+                cross((unit - 6) // 2, 6, 8)
+            if unit % 2 == 1 and on(unit + 3):
+                copy_out()
             if on(unit - 1):
                 copy_out()
             invert_norms(unit)
-            if unit % 2 == 0 and on(unit + 4):
-                copy_out()
             if unit % 2 == 0:
                 load_tokens((unit - 1) // 2 + 3)
             else:

from contextlib import ExitStack

import concourse.mybir as mybir
from concourse.masks import make_identity

F32 = mybir.dt.float32
BF16 = mybir.dt.bfloat16
U32 = mybir.dt.uint32
U8 = mybir.dt.uint8
FP8X4 = mybir.dt.float8_e4m3fn_x4
ALU = mybir.AluOpType
ACT = mybir.ActivationFunctionType
AXIS = mybir.AxisListType

P = 128
PACK = 4
EXPERTS = 8
HALVES = 2
STEPS = EXPERTS * HALVES
TOKENS = 8
SEGMENTS = 2
UNITS = STEPS * SEGMENTS
INNER = 2
SLOTS = INNER * SEGMENTS
D = 512
WORDS = D // 2
T = 8
B = 16
QUAD = 32
QUAD_GROUPS = QUAD // TOKENS
CROSS_COLUMNS = 128
PARTS = ((0, 8),)
AHEAD = 2
FIRST_PASSES = 2
EPS = 1e-6

FLOPS = 2 * STEPS * P * SEGMENTS * D * INNER * D + 2 * STEPS * P * TOKENS * SLOTS * D


def tile_hierarchicalsoftmoe2dblock_pb_t_kernel(tc, yn, means, w_slot2, out_0, out_1):
    nc = tc.nc
    yn_rows = yn.rearrange("b g k s d -> k (b g) (s d)")
    means_rows = means.rearrange("b g k m d -> k (b g) (m d)")

    with ExitStack() as ctx:
        consts = ctx.enter_context(tc.tile_pool(name="consts", bufs=1))
        w_pool = ctx.enter_context(tc.tile_pool(name="w_pool", bufs=3))
        m_pool = ctx.enter_context(tc.tile_pool(name="m_pool", bufs=4))
        y_pool = ctx.enter_context(tc.tile_pool(name="y_pool", bufs=4))
        w_ring = ctx.enter_context(tc.tile_pool(name="w_ring", bufs=2))
        two = ctx.enter_context(tc.tile_pool(name="two", bufs=2))
        three = ctx.enter_context(tc.tile_pool(name="three", bufs=3))
        small = ctx.enter_context(tc.tile_pool(name="small", bufs=4))
        last = ctx.enter_context(tc.tile_pool(name="last", bufs=2))
        turned_ps = ctx.enter_context(tc.psum_pool(name="turned_ps", bufs=3))
        rows_ps = ctx.enter_context(tc.psum_pool(name="rows_ps", bufs=4))
        logit_ps = ctx.enter_context(tc.psum_pool(name="logit_ps", bufs=1))
        ctx.enter_context(tc.manual_schedule())

        w_raw, m_raw, y_raw = {}, {}, {}
        w_grouped, w_codes, w_scales = {}, {}, {}
        m_grouped, m_codes, m_scales = {}, {}, {}
        y_grouped, y_codes, y_scales = {}, {}, {}
        s_grouped, s_codes, s_scales = {}, {}, {}
        se_banks, square_sums, inv_norms, se2_rows, crossed = {}, {}, {}, {}, {}
        m_turned, y_turned, s_turned = {}, {}, {}
        spread, tops, shifteds, totals = {}, {}, {}, {}

        def load_w(k, part=0, parts=1):
            if not 0 <= k < EXPERTS:
                return
            if part == 0:
                w_in = w_pool.tile([P, PACK, INNER * D], BF16)
                w_raw[k] = w_in
            width = INNER * D // parts
            cols = slice(part * width, (part + 1) * width)
            nc.sync.dma_start(
                out=w_raw[k][:, :, cols], in_=w_slot2[k].rearrange("(p j) c -> p j c", j=PACK)[:, :, cols]
            )

        def load_means(n):
            if not 0 <= n < STEPS:
                return
            k, h = divmod(n, HALVES)
            m_in = m_pool.tile([P, SEGMENTS * D], BF16)
            nc.sync.dma_start(out=m_in[:], in_=means_rows[k, h * P : (h + 1) * P, :])
            m_raw[n] = m_in

        def load_tokens(n, part=0, parts=1):
            if not 0 <= n < STEPS:
                return
            k, h = divmod(n, HALVES)
            if part == 0:
                y_in = y_pool.tile([P, TOKENS * D], BF16)
                y_raw[n] = y_in
            cols = slice(part * TOKENS * D // parts, (part + 1) * TOKENS * D // parts)
            nc.sync.dma_start(out=y_raw[n][:, cols], in_=yn_rows[k, h * P : (h + 1) * P, cols])

        def regroup_w(k, i, engine):
            if not 0 <= k < EXPERTS:
                return
            e, part = divmod(i, 2)
            width = D // 2
            w_new = w_ring.tile([P, width * PACK], BF16, align_bytes=64, name="w_grouped")
            w_grouped[k, i] = w_new
            dst = w_new[:]
            src = w_raw[k][:, :, i * width : (i + 1) * width]
            if engine == nc.gpsimd:
                nc.gpsimd.tensor_scalar(
                    out=dst.rearrange("p (c j) -> p c j", j=PACK),
                    in0=src.rearrange("p j c -> p c j"),
                    scalar1=1.0,
                    scalar2=0.0,
                    op0=ALU.mult,
                    op1=ALU.add,
                )
                return
            copy = nc.scalar.copy if engine == nc.scalar else nc.vector.tensor_copy
            copy(out=dst.rearrange("p (c j) -> p c j", j=PACK), in_=src.rearrange("p j c -> p c j"))

        def quantise_quarter(k, i):
            if not 0 <= k < EXPERTS:
                return
            e, part = divmod(i, 2)
            if part == 0:
                codes = two.tile([P, D], U32, align_bytes=64, name="w_codes%d" % e)
                scales = two.tile([P, D], U8, align_bytes=64, name="w_scales%d" % e)
                w_codes[k, e], w_scales[k, e] = codes, scales
            cols = slice(part * D // 2, (part + 1) * D // 2)
            nc.vector.quantize_mx(
                out=w_codes[k, e][:, cols].bitcast(FP8X4), scales=w_scales[k, e][:, cols], in_=w_grouped[k, i][:]
            )

        def turn_means(n):
            words = m_raw[n][:].bitcast(F32)
            turned = turned_ps.tile([P, SEGMENTS, 2, P], F32)
            for m in range(SEGMENTS):
                for u in range(2):
                    nc.tensor.transpose(
                        turned[:, m, u, :], words[:, m * WORDS + u : (m + 1) * WORDS : 2], ident[:]
                    )
            m_turned[n] = turned

        def copy_means(n):
            m_new = two.tile([P, SEGMENTS * P * PACK], BF16, align_bytes=64, name="m_grouped")
            engine = nc.scalar.copy if n < 2 else nc.vector.tensor_copy
            engine(
                out=m_new[:].bitcast(F32).rearrange("p (m c u) -> p m c u", c=P, u=2),
                in_=m_turned[n][:].rearrange("p m u c -> p m c u"),
            )
            m_grouped[n] = m_new

        def quantise_means(n):
            if not 0 <= n < STEPS:
                return
            codes = three.tile([P, SEGMENTS * P], U32, align_bytes=64, name="m_codes")
            scales = three.tile([P, SEGMENTS * P], U8, align_bytes=64, name="m_scales")
            nc.vector.quantize_mx(out=codes[:].bitcast(FP8X4), scales=scales[:], in_=m_grouped[n][:])
            m_codes[n], m_scales[n] = codes, scales

        def turn_tokens(n, i):
            words = y_raw[n][:].bitcast(F32)
            turned = turned_ps.tile([P, 2, 2, P], F32)
            for s in range(2):
                for u in range(2):
                    row = 2 * i + s
                    nc.tensor.transpose(turned[:, s, u, :], words[:, row * WORDS + u : (row + 1) * WORDS : 2], ident[:])
            y_turned[n, i] = turned

        def copy_tokens(n, i):
            if i == 0:
                y_new = two.tile([P, P * TOKENS * PACK], BF16, align_bytes=64, name="y_grouped")
                y_grouped[n] = y_new
            pairs = y_grouped[n][:].bitcast(F32).rearrange("p (g s u) -> p g s u", s=TOKENS, u=2)
            engine = nc.vector.tensor_copy if i == 2 else nc.scalar.copy
            engine(
                out=pairs[:, :, 2 * i : 2 * i + 2, :], in_=y_turned[n, i][:].rearrange("p s u g -> p g s u")
            )

        def quantise_tokens(n):
            codes = three.tile([P, T * P], U32, align_bytes=64, name="y_codes")
            scales = three.tile([P, T * P], U8, align_bytes=64, name="y_scales")
            nc.vector.quantize_mx(out=codes[:].bitcast(FP8X4), scales=scales[:], in_=y_grouped[n][:])
            y_codes[n], y_scales[n] = codes, scales

        def multiply_means(unit, e):
            if not 0 <= unit < UNITS:
                return
            n, m = divmod(unit, SEGMENTS)
            k = n // HALVES
            se = rows_ps.tile([P, D], F32)
            for again in range(FIRST_PASSES):
                nc.tensor.matmul_mx(
                    out=se[:],
                    lhsT=m_codes[n][:, m * P : (m + 1) * P].bitcast(FP8X4),
                    lhsT_scale=m_scales[n][:, m * P : (m + 1) * P],
                    rhs=w_codes[k, e][:].bitcast(FP8X4),
                    rhs_scale=w_scales[k, e][:],
                    start=True,
                    stop=True,
                )
            se_banks[unit, e] = se

        def sum_squares(unit, e):
            if not 0 <= unit < UNITS:
                return
            if e == 0:
                sums = small.tile([P, INNER], F32)
                square_sums[unit] = sums
            squares = small.tile([P, D], BF16)
            nc.scalar.activation(
                out=squares[:], in_=se_banks[unit, e][:], func=ACT.Square, accum_out=square_sums[unit][:, e : e + 1]
            )

        def invert_norms(unit):
            if not 0 <= unit < UNITS:
                return
            inv_norm = small.tile([P, INNER], F32)
            nc.scalar.activation(
                out=inv_norm[:],
                in_=square_sums[unit][:],
                func=ACT.Abs_reciprocal_sqrt,
                scale=1.0 / D,
                bias=EPS / D,
            )
            inv_norms[unit] = inv_norm

        def normalise(unit, e, on_scalar):
            if not 0 <= unit < UNITS:
                return
            if e == 0:
                rows = two.tile([P, INNER * D], BF16, name="se2_rows")
                se2_rows[unit] = rows
            out = se2_rows[unit][:, e * D : (e + 1) * D].rearrange("p (u q o) -> p u q o", u=2, o=2)
            in_ = se_banks[unit, e][:].rearrange("p (q u o) -> p u q o", u=2, o=2)
            if on_scalar:
                nc.scalar.activation(out=out, in_=in_, func=ACT.Copy, scale=inv_norms[unit][:, e : e + 1])
            else:
                nc.vector.tensor_scalar(
                    out=out, in0=in_, scalar1=inv_norms[unit][:, e : e + 1], scalar2=None, op0=ALU.mult
                )

        def turn_slots(unit):
            words = se2_rows[unit][:].bitcast(F32)
            turned = turned_ps.tile([P, INNER, 2, P], F32)
            for e in range(INNER):
                for u in range(2):
                    first = e * WORDS + u * P
                    nc.tensor.transpose(turned[:, e, u, :], words[:, first : first + P], ident[:])
            s_turned[unit] = turned

        def copy_slots(unit):
            n, m = divmod(unit, SEGMENTS)
            if m == 0:
                s_new = two.tile([P, P * SLOTS * PACK], BF16, align_bytes=64, name="s_grouped")
                s_grouped[n] = s_new
            pairs = s_grouped[n][:].bitcast(F32).rearrange("p (g m e u) -> p m g e u", m=SEGMENTS, e=INNER, u=2)
            nc.scalar.copy(out=pairs[:, m], in_=s_turned[unit][:].rearrange("p e u g -> p g e u"))

        def quantise_slots(n):
            if not 0 <= n < STEPS:
                return
            codes = two.tile([P, P * SLOTS], U32, align_bytes=64, name="s_codes")
            scales = two.tile([P, P * SLOTS], U8, align_bytes=64, name="s_scales")
            nc.vector.quantize_mx(out=codes[:].bitcast(FP8X4), scales=scales[:], in_=s_grouped[n][:])
            s_codes[n], s_scales[n] = codes, scales

        def cross(n, t0, t1):
            if not 0 <= n < STEPS:
                return
            if t0 == 0:
                pool, bank = (logit_ps, "crossed") if n < STEPS - 2 else (rows_ps, "se")
                crossed_new = pool.tile([P, T * B * SLOTS], F32, name=bank)
                crossed[n] = crossed_new
            for t in range(t0, t1):
                first = t * B * SLOTS
                width = B * SLOTS
                while width < CROSS_COLUMNS and first + 2 * width <= T * B * SLOTS:
                    width *= 2
                cols = slice(first, first + width)
                nc.tensor.matmul_mx(
                    out=crossed[n][:, cols],
                    lhsT=y_codes[n][:, t * P : (t + 1) * P].bitcast(FP8X4),
                    lhsT_scale=y_scales[n][:, t * P : (t + 1) * P],
                    rhs=s_codes[n][:, cols].bitcast(FP8X4),
                    rhs_scale=s_scales[n][:, cols],
                    start=True,
                    stop=True,
                )

        def pick(n):
            if not 0 <= n < STEPS:
                return
            k, h = divmod(n, HALVES)
            part = [k0 <= k < k1 for k0, k1 in PARTS].index(True)
            first = ((k - PARTS[part][0]) * HALVES + h) * T
            by_group = crossed[n][:].rearrange("q (t b x) -> q x b t", t=T, b=B)
            for a in range(P // QUAD):
                rows = slice(a * QUAD, (a + 1) * QUAD)
                groups = slice(a * QUAD_GROUPS, (a + 1) * QUAD_GROUPS)
                nc.scalar.copy(out=candidates[part][rows, :, :, first : first + T], in_=by_group[rows, :, groups, :])

        def spread_part(part, j):
            k0, k1 = PARTS[part]
            width = (k1 - k0) * HALVES * T
            span = P // width
            if j >= QUAD_GROUPS // span:
                return
            if j == 0:
                x = last.tile([P, SLOTS, B // span, TOKENS], F32, name="spread")
                spread[part] = x
            turned = turned_ps.tile([P, SLOTS, P], F32)
            flat = candidates[part][:].rearrange("q x c r -> q x (c r)")
            for slot in range(SLOTS):
                e, m = divmod(slot, SEGMENTS)
                nc.tensor.transpose(turned[:, slot, :], flat[:, INNER * m + e, j * P : (j + 1) * P], ident[:])
            by_c = turned[:].rearrange("r slot (a c s) -> r slot c a s", c=QUAD_GROUPS, s=TOKENS)
            chosen = spread[part][:].rearrange("r slot (a j) s -> r slot j a s", j=QUAD_GROUPS // span)
            for c in range(span):
                rows = slice(c * width, (c + 1) * width)
                nc.vector.tensor_copy(out=chosen[rows, :, j], in_=by_c[rows, :, span * j + c])

        def softmax_views(part):
            groups = spread[part].shape[2]
            full = [P, SLOTS, groups, TOKENS]
            over_tokens = (out_0, lambda x: x, [P, SLOTS, groups], lambda x: x.unsqueeze(3).to_broadcast(full))
            over_slots = (
                out_1,
                lambda x: x.rearrange("r slot g s -> r g s slot"),
                [P, groups, TOKENS],
                lambda x: x.unsqueeze(1).to_broadcast(full),
            )
            return over_tokens, over_slots

        def find_tops(part):
            for i, (out, index_last, reduced_shape, repeated) in enumerate(softmax_views(part)):
                top = last.tile(reduced_shape, F32, name="top%d" % i)
                nc.vector.tensor_reduce(out=top[:], in_=index_last(spread[part][:]), axis=AXIS.X, op=ALU.max)
                tops[part, i] = top

        def exponentiate(part):
            for i, (out, index_last, reduced_shape, repeated) in enumerate(softmax_views(part)):
                shifted = last.tile(spread[part].shape, F32, name="shifted%d" % i)
                nc.vector.tensor_tensor(
                    out=shifted[:], in0=spread[part][:], in1=repeated(tops[part, i][:]), op=ALU.subtract
                )
                nc.scalar.activation(out=shifted[:], in_=shifted[:], func=ACT.Exp)
                shifteds[part, i] = shifted

        def invert_totals(part):
            for i, (out, index_last, reduced_shape, repeated) in enumerate(softmax_views(part)):
                total = last.tile(reduced_shape, F32, name="total%d" % i)
                nc.vector.tensor_reduce(out=total[:], in_=index_last(shifteds[part, i][:]), axis=AXIS.X, op=ALU.add)
                nc.vector.reciprocal(out=total[:], in_=total[:])
                totals[part, i] = total

        def finish(part, queues):
            k0, k1 = PARTS[part]
            rows = HALVES * T
            span = P // ((k1 - k0) * rows)
            for i, (out, index_last, reduced_shape, repeated) in enumerate(softmax_views(part)):
                weights = last.tile([P, B // span, TOKENS, SLOTS], F32, name="weights%d" % i)
                nc.vector.tensor_tensor(
                    out=weights[:],
                    in0=shifteds[part, i][:].rearrange("r slot g s -> r g s slot"),
                    in1=repeated(totals[part, i][:]).rearrange("r slot g s -> r g s slot"),
                    op=ALU.mult,
                )
                per_expert = out.rearrange("x g k s slot -> k (x g) (s slot)")
                for c in range(span):
                    for k in range(k0, k1):
                        first = (c * (k1 - k0) + k - k0) * rows
                        queues[i].dma_start(
                            out=per_expert[k].rearrange("(r g c) w -> c r g w", c=span, r=rows)[c],
                            in_=weights[first : first + rows].rearrange("r g s slot -> r g (s slot)"),
                        )

        one = consts.tile([P, 1], F32)
        nc.vector.memset(one[:], 1.0)
        nc.scalar.activation(out=one[:], in_=one[:], func=ACT.Abs_reciprocal_sqrt)
        ident = consts.tile([P, P], F32)
        make_identity(nc, ident[:])
        candidates = []
        for part, (k0, k1) in enumerate(PARTS):
            held = consts.tile([P, SLOTS, QUAD_GROUPS, (k1 - k0) * HALVES * T], F32, name="candidates%d" % part)
            candidates.append(held)

        uses = [(turn_means, copy_means, (0,)), (turn_means, copy_means, (1,))]

        def on(unit):
            return 0 <= unit < UNITS

        def listed(turn, copy, *args):
            uses.append((turn, copy, args))

        for unit in range(UNITS + 8):
            if on(unit - 1):
                listed(turn_tokens, copy_tokens, (unit - 1) // 2, 2 * ((unit - 1) % 2))
            if on(unit - 2):
                listed(turn_slots, copy_slots, unit - 2)
            if unit % 2 == 1 and on(unit + 3):
                listed(turn_means, copy_means, unit // 2 + 2)
            if on(unit - 1):
                listed(turn_tokens, copy_tokens, (unit - 1) // 2, 2 * ((unit - 1) % 2) + 1)
        done = [0, 0]

        def copy_out(ahead=AHEAD):
            while done[0] < min(done[1] + ahead + 1, len(uses)):
                turn, copy, args = uses[done[0]]
                if turn == turn_slots and args[0] not in se2_rows:
                    break
                turn(*args)
                done[0] += 1
            turn, copy, args = uses[done[1]]
            copy(*args)
            done[1] += 1

        load_w(0, 0, 4)
        load_w(0, 1, 4)
        load_means(0)
        load_w(0, 1, 2)
        load_means(1)
        load_tokens(0, 0, 2)
        load_w(1, 0, 2)
        load_means(2)
        load_tokens(0, 1, 2)
        load_w(1, 1, 2)
        load_tokens(1)
        load_means(3)
        load_w(2)
        regroup_w(0, 0, nc.vector)
        regroup_w(0, 1, nc.scalar)
        copy_out(1)
        quantise_quarter(0, 0)
        quantise_quarter(0, 1)
        quantise_means(0)
        multiply_means(0, 0)
        regroup_w(0, 2, nc.vector)
        regroup_w(0, 3, nc.scalar)
        quantise_quarter(0, 2)
        quantise_quarter(0, 3)
        multiply_means(0, 1)
        copy_out(1)
        quantise_means(1)
        regroup_w(1, 0, nc.vector)
        regroup_w(1, 1, nc.gpsimd)

        for unit in range(UNITS + 8):
            sum_squares(unit, 0)
            if (unit - 5) % 2 == 0:
                quantise_slots((unit - 5) // 2)
            if on(unit - 4) and unit % 2 == 0:
                quantise_tokens(unit // 2 - 2)
            if unit % 2 == 0 and unit > 0:
                quantise_means(unit // 2 + 1)
            quantise_quarter((unit + 4) // 4, (unit + 4) % 4)
            regroup_w((unit + 2) // 4 + 1, (unit + 2) % 4, nc.gpsimd)
            if unit > 0:
                multiply_means(unit, 1)
            if (unit - 6) % 2 == 0:
                cross((unit - 6) // 2, 3, 6)
            if on(unit - 1):
                copy_out()
            if on(unit - 2):
                copy_out()
            normalise(unit - 1, 0, False)
            normalise(unit - 1, 1, False)
            if (unit - 7) % 2 == 0:
                pick((unit - 7) // 2)
            sum_squares(unit, 1)
            multiply_means(unit + 1, 0)
            if (unit - 5) % 2 == 0:
                cross((unit - 5) // 2, 0, 3)
            if (unit - 6) % 2 == 0:
                cross((unit - 6) // 2, 6, 8)
            if unit % 2 == 1 and on(unit + 3):
                copy_out()
            if on(unit - 1):
                copy_out()
            invert_norms(unit)
            if unit % 2 == 0:
                load_tokens((unit - 1) // 2 + 3)
            else:
                load_means(unit // 2 + 4)
                if unit % 4 == 3:
                    load_w(unit // 4 + 3)

        end = len(PARTS) - 1
        for j in range(QUAD_GROUPS):
            spread_part(end, j)
        find_tops(end)
        exponentiate(end)
        invert_totals(end)
        finish(end, (nc.sync, nc.scalar))
